import numpy as np
import ml_dtypes


def mxq(x, axis, fmt="e4m3"):
    dtype, down = {"e4m3": (ml_dtypes.float8_e4m3fn, 7), "e5m2": (ml_dtypes.float8_e5m2, 14)}[fmt]
    v = np.moveaxis(np.asarray(x, np.float32).astype(ml_dtypes.bfloat16).astype(np.float64), axis, -1)
    blocks = v.reshape(v.shape[:-1] + (-1, 32))
    amax = np.abs(blocks).max(-1, keepdims=True)
    byte = np.maximum(np.where(amax > 0, np.frexp(amax)[1] - 1 + 127, 0) - down, 1)
    scale = np.exp2(byte - 127.0)
    codes = (blocks / scale).astype(np.float32).astype(dtype).astype(np.float64)
    return np.moveaxis((codes * scale).reshape(v.shape), -1, axis)


WIDE = False


def mx_kscale(k):
    if not WIDE:
        return np.ones(k)
    levels = np.array([10, -10, 5, -5, 0])
    if k % 512:
        return np.exp2(np.random.permutation(np.resize(levels, k // 32))).repeat(32)
    a = np.empty((k // 512, 16))
    for p in range(k // 512):
        a[p, :8] = np.random.permutation(np.resize(levels, 8))
        for g in range(8):
            far = levels[np.abs(levels - a[p, g]) >= 10]
            a[p, g + 8] = far[np.random.randint(len(far))]
    return np.exp2(a.ravel()).repeat(32)


BF16 = ml_dtypes.bfloat16


def bf(x):
    return np.asarray(x, np.float32).astype(BF16)


def f64(x):
    return np.asarray(x).astype(np.float64)


B, NV, S, D, H = 2, 8, 512, 512, 8
HD = D // H


def setup_inputs():
    s, t = mx_kscale(D), mx_kscale(D)
    return {"x": bf(np.random.standard_normal((B * NV, S, D)) * s),
            "scores": bf(np.random.standard_normal((B, NV, NV, H, S)) * 1.4),
            "Wv": bf(np.random.standard_normal((D, D)) / np.sqrt(D) / s[:, None] * t),
            "bv": bf(np.random.standard_normal(D) * 0.3 * t),
            "Wo": bf(np.random.standard_normal((D, D)) / np.sqrt(D) / t[:, None]),
            "bo": bf(np.random.standard_normal(D) * 0.3)}


def reference(x, scores, Wv, bv, Wo, bo):
    v = (mxq(f64(x), 2, "e4m3") @ mxq(f64(Wv), 0, "e4m3")) + f64(bv)
    v = v.reshape(B, NV, S, H, HD).transpose(0, 1, 3, 2, 4)
    sc = f64(scores)
    e = np.exp(sc - sc.max(2, keepdims=True))
    w = e / e.sum(2, keepdims=True)
    mixed = np.zeros((B, NV, H, S, HD))
    for j in range(NV):
        mixed = mixed + w[:, :, j, :, :, None] * v[:, j][:, None]
    mixed = mixed.transpose(0, 1, 3, 2, 4).reshape(B * NV, S, D)
    return (mxq(mixed, 2, "e4m3") @ mxq(f64(Wo), 0, "e4m3")) + f64(bo)

@@ -1,0 +1,406 @@
+from contextlib import ExitStack
+
+import concourse.mybir as mybir
+from concourse.masks import make_identity
+
+F32 = mybir.dt.float32
+BF16 = mybir.dt.bfloat16
+U32 = mybir.dt.uint32
+U8 = mybir.dt.uint8
+FP8X4 = mybir.dt.float8_e4m3fn_x4
+ALU = mybir.AluOpType
+ACT = mybir.ActivationFunctionType
+
+P = 128
+PACK = 4
+B = 2
+NV = 8
+S = 512
+D = 512
+H = 8
+HD = D // H
+T = P // NV
+G = S // T
+OCT = 8
+N_OCT = G // OCT
+TENSOR_OCTS = 2
+TENSOR_TILES = TENSOR_OCTS * OCT
+VECTOR_OCTS = N_OCT - TENSOR_OCTS
+LEAD = 4
+STORE = 2
+
+FLOPS = 2 * 2 * B * NV * S * D * D + 2 * B * NV * NV * S * D
+
+
+def quantise_weight(nc, setup, keep, name, load_rows):
+    raw = setup.tile([P, PACK, D], BF16, name="w_raw")
+    load_rows(raw)
+    grouped = setup.tile([P, D, PACK], BF16, name="w_grouped", align_bytes=64)
+    nc.vector.tensor_copy(out=grouped[:], in_=raw[:].rearrange("p a c -> p c a"))
+    codes = keep.tile([P, D], U32, name=name + "_codes", align_bytes=64)
+    scales = keep.tile([P, D], U8, name=name + "_scales", align_bytes=64)
+    nc.vector.quantize_mx(
+        out=codes[:].bitcast(FP8X4), scales=scales[:], in_=grouped[:].rearrange("p c a -> p (c a)")
+    )
+    return codes, scales
+
+
+def load_scores(nc, setup, scores):
+    raw = setup.tile([P, NV, S], BF16, name="scores_raw")
+    for h in range(H):
+        nc.sync.dma_start(
+            out=raw[h * B * NV : (h + 1) * B * NV, :, :],
+            in_=scores[:, :, :, h, :].rearrange("b i j s -> (b i) j s"),
+        )
+    return raw
+
+
+def softmax_exponentials(nc, soft, raw, o):
+    part = raw[:].rearrange("p j (t o r) -> p o j t r", t=T, o=N_OCT, r=OCT)[:, o, :, :, :]
+    top = soft.tile([P, NV // 2, T, OCT], BF16, name="top")
+    nc.vector.tensor_max(out=top[:], in0=part[:, 0:4, :, :], in1=part[:, 4:8, :, :])
+    nc.vector.tensor_max(out=top[:, 0:2, :, :], in0=top[:, 0:2, :, :], in1=top[:, 2:4, :, :])
+    nc.vector.tensor_max(out=top[:, 0:1, :, :], in0=top[:, 0:1, :, :], in1=top[:, 1:2, :, :])
+    e = soft.tile([P, NV, T, OCT], F32, name="e")
+    nc.vector.tensor_tensor(
+        out=e[:], in0=part, in1=top[:, 0:1, :, :].to_broadcast([P, NV, T, OCT]), op=ALU.subtract
+    )
+    nc.scalar.activation(out=e[:], in_=e[:], func=ACT.Exp)
+    return e
+
+
+def softmax_weights(nc, soft, e, order, shape):
+    total = soft.tile([P, NV // 2, T, OCT], F32, name="total")
+    nc.vector.tensor_add(out=total[:], in0=e[:, 0:4, :, :], in1=e[:, 4:8, :, :])
+    nc.vector.tensor_add(out=total[:, 0:2, :, :], in0=total[:, 0:2, :, :], in1=total[:, 2:4, :, :])
+    nc.vector.tensor_add(out=total[:, 0:1, :, :], in0=total[:, 0:1, :, :], in1=total[:, 1:2, :, :])
+    nc.vector.reciprocal(out=total[:, 0:1, :, :], in_=total[:, 0:1, :, :])
+    w = soft.tile([P] + shape, F32, name="w")
+    nc.vector.tensor_tensor(
+        out=w[:],
+        in0=e[:].rearrange("p j t r -> p " + order),
+        in1=total[:, 0:1, :, :].rearrange("p j t r -> p " + order).to_broadcast([P] + shape),
+        op=ALU.mult,
+    )
+    return w
+
+
+def tile_crossviewattention_pa_t_kernel(tc, x, scores, Wv, bv, Wo, bo, out):
+    nc = tc.nc
+    x_tiles = x.flatten_outer_dims().rearrange("(b p g) d -> b p g d", b=B, p=P, g=G)
+    out_tiles = out.flatten_outer_dims().rearrange("(b p g) d -> b p g d", b=B, p=P, g=G)
+
+    with ExitStack() as stack:
+        keep = stack.enter_context(tc.tile_pool(name="keep", bufs=1))
+        setup = stack.enter_context(tc.tile_pool(name="setup", bufs=1))
+        soft = stack.enter_context(tc.tile_pool(name="soft", bufs=2))
+        two = stack.enter_context(tc.tile_pool(name="two", bufs=2))
+        flow = stack.enter_context(tc.tile_pool(name="flow", bufs=4))
+        waiting = stack.enter_context(tc.tile_pool(name="waiting", bufs=6))
+        ps_view = stack.enter_context(tc.psum_pool(name="ps_view", bufs=2))
+        ps_v = stack.enter_context(tc.psum_pool(name="ps_v", bufs=1))
+        ps_mix = stack.enter_context(tc.psum_pool(name="ps_mix", bufs=1))
+        ps_y = stack.enter_context(tc.psum_pool(name="ps_y", bufs=2))
+        ps_turn = stack.enter_context(tc.psum_pool(name="ps_turn", bufs=2))
+
+        ident_f32 = keep.tile([P, P], F32, name="ident_f32")
+        make_identity(nc, ident_f32[:])
+        same_t_once = keep.tile([P, T], F32, name="same_t_once")
+        nc.vector.tensor_reduce(
+            out=same_t_once[:],
+            in_=ident_f32[:].rearrange("p (j t) -> p t j", j=NV, t=T),
+            axis=mybir.AxisListType.X,
+            op=ALU.add,
+        )
+        same_t = keep.tile([P, T, NV], F32, name="same_t")
+        nc.vector.tensor_copy(out=same_t[:], in_=same_t_once[:].unsqueeze(2).to_broadcast([P, T, NV]))
+
+        octet_order = [o + k for k in range(TENSOR_OCTS) for o in (0, TENSOR_OCTS)]
+        x_order = [(b, o) for b in range(B) for k in range(TENSOR_OCTS) for o in (TENSOR_OCTS + k, k)]
+        x_loaded = {}
+        x_mx = {}
+
+        def load_x(n):
+            b, o = x_order[n]
+            x_oct = two.tile([P, OCT * D], BF16, name="x_oct")
+            nc.sync.dma_start(
+                out=x_oct[:],
+                in_=x_tiles[b, :, o * OCT : (o + 1) * OCT, :].rearrange("p r d -> p (r d)"),
+            )
+            x_loaded[n] = x_oct
+
+        def prepare_x(n):
+            b, o = x_order[n]
+            x_words = x_loaded[n][:].bitcast(F32)
+            xg = keep.tile([P, OCT * P * PACK], BF16, name="xg", align_bytes=64)
+            xg_words = xg[:].bitcast(F32)
+            by_tile = xg_words.rearrange("p (r n u) -> p r n u", r=OCT, n=P, u=2)
+            by_view = xg_words.rearrange("p (j r t u) -> p j r t u", j=NV, r=OCT, t=T, u=2)
+            for r0 in range(0, OCT, 2):
+                xt = ps_turn.tile([P, 2, 2, P], F32, tag="turn", name="xt")
+                for k in range(2):
+                    for u in range(2):
+                        first = (r0 + k) * (D // 2)
+                        nc.tensor.transpose(
+                            out=xt[:, k, u, :],
+                            in_=x_words[:, first + u : first + D // 2 : 2],
+                            identity=ident_f32[:],
+                        )
+                if o >= TENSOR_OCTS:
+                    for k in range(2):
+                        nc.scalar.copy(
+                            out=by_view[:, :, r0 + k, :, :],
+                            in_=xt[:, k, :, :].rearrange("p u (j t) -> p j t u", j=NV, t=T),
+                        )
+                else:
+                    nc.scalar.copy(
+                        out=by_tile[:, r0 : r0 + 2, :, :], in_=xt[:].rearrange("p k u n -> p k n u")
+                    )
+            kind = "view" if o >= TENSOR_OCTS else "tile"
+            codes = two.tile([P, OCT * P], U32, name="x_codes_" + kind, align_bytes=64)
+            scales = two.tile([P, OCT * P], U8, name="x_scales_" + kind, align_bytes=64)
+            nc.vector.quantize_mx(out=codes[:].bitcast(FP8X4), scales=scales[:], in_=xg[:])
+            x_mx[(b, o)] = (codes, scales)
+            if n + 2 < len(x_order):
+                load_x(n + 2)
+
+        def load_wv(raw):
+            nc.scalar.dma_start(out=raw[:], in_=Wv.rearrange("(p a) c -> p a c", a=PACK))
+
+        def load_wo(raw):
+            nc.scalar.dma_start(out=raw[:], in_=Wo.rearrange("(p a) c -> p a c", a=PACK))
+
+        w_rows = keep.tile([P, TENSOR_TILES, P], F32, name="w_rows")
+        w_cols = keep.tile([P, VECTOR_OCTS, NV, P], F32, name="w_cols")
+        w_by_scene = w_rows[:].rearrange("p g (h b i) -> p b g h i", h=H, b=B, i=NV)
+
+        def spread_weights(o, e):
+            if o >= TENSOR_OCTS:
+                w = softmax_weights(nc, soft, e, "j r t", [NV, OCT, T])
+                turned = w_cols[:, o - TENSOR_OCTS, :, :]
+            else:
+                w = softmax_weights(nc, soft, e, "r j t", [OCT, NV, T])
+                turned = w_rows[:, o * OCT : (o + 1) * OCT, :]
+            for first in range(0, OCT, 4):
+                wt = ps_turn.tile([P, 4, P], F32, tag="turn", name="wt")
+                for k in range(4):
+                    nc.tensor.transpose(
+                        out=wt[:, k, :],
+                        in_=w[:, first + k, :, :].rearrange("p m n -> p (m n)"),
+                        identity=ident_f32[:],
+                    )
+                nc.scalar.copy(out=turned[:, first : first + 4, :], in_=wt[:])
+
+        mixers = stack.enter_context(tc.tile_pool(name="mixers", bufs=LEAD + 2))
+        mixer_of = {}
+
+        def stage_mixers(n):
+            b, g = divmod(n, TENSOR_TILES)
+            mixer = mixers.tile([P, H, T, NV], F32, name="mixer")
+            nc.gpsimd.tensor_tensor(
+                out=mixer[:],
+                in0=w_by_scene[:, b, g, :, :].unsqueeze(2).to_broadcast([P, H, T, NV]),
+                in1=same_t[:].unsqueeze(1).to_broadcast([P, H, T, NV]),
+                op=ALU.mult,
+            )
+            mixer_of[n] = mixer
+
+        def project(pool, operand, first, weight):
+            codes, scales = operand
+            w_codes, w_scales = weight
+            tokens = slice(first, first + P)
+            sums = pool.tile([P, D], F32, name="sums")
+            nc.tensor.matmul_mx(
+                out=sums[:],
+                lhsT=codes[:, tokens].bitcast(FP8X4),
+                lhsT_scale=scales[:, tokens],
+                rhs=w_codes[:].bitcast(FP8X4),
+                rhs_scale=w_scales[:],
+                start=True,
+                stop=True,
+            )
+            return sums
+
+        n_tiles = B * TENSOR_TILES
+        v_of = {}
+        mixed_of = {}
+        grouped_of = {}
+        m_mx_of = {}
+        y_sb_of = {}
+
+        def stage_v(n):
+            b, g = divmod(n, TENSOR_TILES)
+            v = project(ps_v, x_mx[(b, g // OCT)], (g % OCT) * P, wv_mx)
+            v_sb = flow.tile([P, D], F32, name="v_sb")
+            nc.scalar.copy(out=v_sb[:], in_=v[:])
+            nc.gpsimd.tensor_tensor(out=v_sb[:], in0=v_sb[:], in1=bv_all[:], op=ALU.add)
+            v_of[n] = v_sb
+
+        def stage_mix(n):
+            mix = ps_mix.tile([P, D], F32, name="mix")
+            for h in range(H):
+                head = slice(h * HD, (h + 1) * HD)
+                nc.tensor.matmul(
+                    out=mix[:, head],
+                    lhsT=mixer_of[n][:, h, :, :].rearrange("p t i -> p (t i)"),
+                    rhs=v_of[n][:, head],
+                    start=True,
+                    stop=True,
+                )
+            mixed = flow.tile([P, D], BF16, name="mixed")
+            nc.scalar.copy(out=mixed[:], in_=mix[:])
+            mixed_of[n] = mixed
+
+        def turn(mixed_rows):
+            words = mixed_rows.bitcast(F32)
+            mt = ps_turn.tile([P, 2, P], F32, tag="turn", name="mt")
+            for u in range(2):
+                nc.tensor.transpose(out=mt[:, u, :], in_=words[:, u : D // 2 : 2], identity=ident_f32[:])
+            return mt
+
+        def stage_turn(n):
+            mt = turn(mixed_of[n][:])
+            grouped = waiting.tile([P, P * PACK], BF16, name="grouped", align_bytes=64)
+            nc.scalar.copy(
+                out=grouped[:].bitcast(F32).rearrange("p (i t u) -> p i t u", i=NV, t=T, u=2),
+                in_=mt[:].rearrange("p u (t i) -> p i t u", t=T, i=NV),
+            )
+            grouped_of[n] = grouped
+
+        def stage_quantise(n):
+            codes = flow.tile([P, P], U32, name="m_codes", align_bytes=64)
+            scales = flow.tile([P, P], U8, name="m_scales", align_bytes=64)
+            nc.vector.quantize_mx(
+                out=codes[:].bitcast(FP8X4),
+                scales=scales[:],
+                in_=grouped_of[n][:],
+            )
+            m_mx_of[n] = (codes, scales)
+
+        def finish_tile(b, g, operand, first):
+            y = project(ps_y, operand, first, wo_mx)
+            if g % STORE == 0:
+                y_sb_of[(b, g // STORE)] = flow.tile([P, STORE, D], F32, name="y_sb")
+            y_sb = y_sb_of[(b, g // STORE)][:, g % STORE, :]
+            if g < TENSOR_TILES:
+                nc.scalar.copy(out=y_sb, in_=y[:])
+                nc.gpsimd.tensor_tensor(out=y_sb, in0=y_sb, in1=bo_all[:], op=ALU.add)
+            else:
+                nc.vector.tensor_tensor(out=y_sb, in0=y[:], in1=bo_all[:], op=ALU.add)
+            if g % STORE == STORE - 1:
+                nc.sync.dma_start(
+                    out=out_tiles[b, :, g - STORE + 1 : g + 1, :], in_=y_sb_of[(b, g // STORE)][:]
+                )
+
+        n_pairs = B * VECTOR_OCTS * NV
+        view_sums = {}
+        octet_sums = {}
+        octet_mixed = {}
+        octet_grouped = {}
+        octet_mx = {}
+
+        def project_view(k):
+            m, j = divmod(k, NV)
+            octet = (m // VECTOR_OCTS, TENSOR_OCTS + m % VECTOR_OCTS)
+            view_sums[k] = project(ps_view, x_mx[octet], j * P, wv_mx)
+
+        def add_view(k):
+            m, j = divmod(k, NV)
+            b = m // VECTOR_OCTS
+            if j == 0:
+                octet_sums[m] = keep.tile([P, NV, D], F32, name="acc")
+            if j == NV - 1:
+                octet_mixed[m] = keep.tile([P, NV, D], BF16, name="mixed_v")
+            acc = octet_sums[m]
+            for i in range(NV):
+                for h in range(H):
+                    head = slice(h * HD, (h + 1) * HD)
+                    col = (h * B + b) * NV + i
+                    before = bv_all[:, head] if j == 0 else acc[:, i, head]
+                    after = octet_mixed[m][:, i, head] if j == NV - 1 else acc[:, i, head]
+                    nc.vector.scalar_tensor_tensor(
+                        out=after,
+                        in0=view_sums[k][:, head],
+                        scalar=w_cols[:, m % VECTOR_OCTS, j, col : col + 1],
+                        in1=before,
+                        op0=ALU.mult,
+                        op1=ALU.add,
+                    )
+
+        def turn_query_view(m, i):
+            if i == 0:
+                octet_grouped[m] = keep.tile([P, OCT * P * PACK], BF16, name="mgv", align_bytes=64)
+            mt = turn(octet_mixed[m][:, i, :])
+            by_tile = octet_grouped[m][:].bitcast(F32).rearrange(
+                "p (r i t u) -> p r i t u", r=OCT, i=NV, t=T, u=2
+            )
+            nc.scalar.copy(
+                out=by_tile[:, :, i, :, :], in_=mt[:].rearrange("p u (r t) -> p r t u", r=OCT, t=T)
+            )
+
+        def quantise_octet(m):
+            codes = keep.tile([P, OCT * P], U32, name="mv_codes", align_bytes=64)
+            scales = keep.tile([P, OCT * P], U8, name="mv_scales", align_bytes=64)
+            nc.vector.quantize_mx(
+                out=codes[:].bitcast(FP8X4),
+                scales=scales[:],
+                in_=octet_grouped[m][:],
+            )
+            octet_mx[m] = (codes, scales)
+
+        raw_scores = load_scores(nc, setup, scores)
+        load_x(0)
+        load_x(1)
+        wv_mx = quantise_weight(nc, setup, keep, "wv", load_wv)
+        bv_all = keep.tile([P, D], BF16, name="bv_all")
+        nc.scalar.dma_start(out=bv_all[:], in_=bv.partition_broadcast(P))
+        bo_all = keep.tile([P, D], BF16, name="bo_all")
+        nc.scalar.dma_start(out=bo_all[:], in_=bo.partition_broadcast(P))
+        prepare_x(0)
+        exps = {}
+        for k in range(N_OCT + 1):
+            if k < N_OCT:
+                exps[k] = softmax_exponentials(nc, soft, raw_scores, octet_order[k])
+            if k > 0:
+                spread_weights(octet_order[k - 1], exps[k - 1])
+            if k == 1:
+                for n in range(LEAD):
+                    stage_mixers(n)
+                prepare_x(1)
+        wo_mx = quantise_weight(nc, setup, keep, "wo", load_wo)
+        project_view(0)
+        project_view(1)
+        add_view(0)
+
+        for count in range(n_pairs + NV - 1):
+            s = count - 1
+            if 0 <= s - 4 < n_tiles:
+                finish_tile((s - 4) // TENSOR_TILES, (s - 4) % TENSOR_TILES, m_mx_of[s - 4], 0)
+            if 0 <= s + 1 < n_tiles:
+                stage_v(s + 1)
+            if 0 <= s - 3 < n_tiles:
+                stage_quantise(s - 3)
+            if LEAD <= s + LEAD < n_tiles:
+                stage_mixers(s + LEAD)
+            if 0 <= s < n_tiles:
+                stage_mix(s)
+            if count + 2 < n_pairs:
+                project_view(count + 2)
+            since = [count - (NV * m + NV - 1) for m in range(B * VECTOR_OCTS)]
+            for m in range(B * VECTOR_OCTS):
+                if since[m] == NV // 2:
+                    quantise_octet(m)
+            if count + 1 < n_pairs:
+                add_view(count + 1)
+            if 0 <= s - 1 < n_tiles:
+                stage_turn(s - 1)
+            for m in range(B * VECTOR_OCTS):
+                for k in range(2):
+                    if 0 <= since[m] < NV // 2:
+                        turn_query_view(m, 2 * since[m] + k)
+                    if NV // 2 <= since[m] < NV:
+                        r = 2 * (since[m] - NV // 2) + k
+                        g = (TENSOR_OCTS + m % VECTOR_OCTS) * OCT + r
+                        finish_tile(m // VECTOR_OCTS, g, octet_mx[m], r * P)
+            if count % 4 == 1 and 2 + count // 4 < len(x_order):
+                prepare_x(2 + count // 4)

@@ -17,72 +17,29 @@ B = 2
 NV = 8
 S = 512
 D = 512
+WORDS = D // 2
 H = 8
 HD = D // H
 T = P // NV
 G = S // T
 OCT = 8
 N_OCT = G // OCT
-TENSOR_OCTS = 2
+TENSOR_OCTS = 3
 TENSOR_TILES = TENSOR_OCTS * OCT
-VECTOR_OCTS = N_OCT - TENSOR_OCTS
-LEAD = 4
-STORE = 2
+V_OCT = N_OCT - 1
+PAIR = 2
+PAIRS = TENSOR_TILES // PAIR
+N_PAIRS = B * PAIRS
+OCT_PAIRS = OCT // PAIR
+LEAD = 2
+UNITS = 6
+N_UNITS = B * NV * NV
 
 FLOPS = 2 * 2 * B * NV * S * D * D + 2 * B * NV * NV * S * D
 
 
-def quantise_weight(nc, setup, keep, name, load_rows):
-    raw = setup.tile([P, PACK, D], BF16, name="w_raw")
-    load_rows(raw)
-    grouped = setup.tile([P, D, PACK], BF16, name="w_grouped", align_bytes=64)
-    nc.vector.tensor_copy(out=grouped[:], in_=raw[:].rearrange("p a c -> p c a"))
-    codes = keep.tile([P, D], U32, name=name + "_codes", align_bytes=64)
-    scales = keep.tile([P, D], U8, name=name + "_scales", align_bytes=64)
-    nc.vector.quantize_mx(
-        out=codes[:].bitcast(FP8X4), scales=scales[:], in_=grouped[:].rearrange("p c a -> p (c a)")
-    )
-    return codes, scales
-
-
-def load_scores(nc, setup, scores):
-    raw = setup.tile([P, NV, S], BF16, name="scores_raw")
-    for h in range(H):
-        nc.sync.dma_start(
-            out=raw[h * B * NV : (h + 1) * B * NV, :, :],
-            in_=scores[:, :, :, h, :].rearrange("b i j s -> (b i) j s"),
-        )
-    return raw
-
-
-def softmax_exponentials(nc, soft, raw, o):
-    part = raw[:].rearrange("p j (t o r) -> p o j t r", t=T, o=N_OCT, r=OCT)[:, o, :, :, :]
-    top = soft.tile([P, NV // 2, T, OCT], BF16, name="top")
-    nc.vector.tensor_max(out=top[:], in0=part[:, 0:4, :, :], in1=part[:, 4:8, :, :])
-    nc.vector.tensor_max(out=top[:, 0:2, :, :], in0=top[:, 0:2, :, :], in1=top[:, 2:4, :, :])
-    nc.vector.tensor_max(out=top[:, 0:1, :, :], in0=top[:, 0:1, :, :], in1=top[:, 1:2, :, :])
-    e = soft.tile([P, NV, T, OCT], F32, name="e")
-    nc.vector.tensor_tensor(
-        out=e[:], in0=part, in1=top[:, 0:1, :, :].to_broadcast([P, NV, T, OCT]), op=ALU.subtract
-    )
-    nc.scalar.activation(out=e[:], in_=e[:], func=ACT.Exp)
-    return e
-
-
-def softmax_weights(nc, soft, e, order, shape):
-    total = soft.tile([P, NV // 2, T, OCT], F32, name="total")
-    nc.vector.tensor_add(out=total[:], in0=e[:, 0:4, :, :], in1=e[:, 4:8, :, :])
-    nc.vector.tensor_add(out=total[:, 0:2, :, :], in0=total[:, 0:2, :, :], in1=total[:, 2:4, :, :])
-    nc.vector.tensor_add(out=total[:, 0:1, :, :], in0=total[:, 0:1, :, :], in1=total[:, 1:2, :, :])
-    nc.vector.reciprocal(out=total[:, 0:1, :, :], in_=total[:, 0:1, :, :])
-    w = soft.tile([P] + shape, F32, name="w")
-    nc.vector.tensor_tensor(
-        out=w[:],
-        in0=e[:].rearrange("p j t r -> p " + order),
-        in1=total[:, 0:1, :, :].rearrange("p j t r -> p " + order).to_broadcast([P] + shape),
-        op=ALU.mult,
-    )
-    return w
+def by_head(ap):
+    return ap.rearrange("p (u h k) -> p h u k", u=2, h=H, k=HD // 2)
 
 
 def tile_crossviewattention_pa_t_kernel(tc, x, scores, Wv, bv, Wo, bo, out):
@@ -92,118 +49,141 @@ def tile_crossviewattention_pa_t_kernel(tc, x, scores, Wv, bv, Wo, bo, out):
 
     with ExitStack() as stack:
         keep = stack.enter_context(tc.tile_pool(name="keep", bufs=1))
-        setup = stack.enter_context(tc.tile_pool(name="setup", bufs=1))
         soft = stack.enter_context(tc.tile_pool(name="soft", bufs=2))
-        two = stack.enter_context(tc.tile_pool(name="two", bufs=2))
-        flow = stack.enter_context(tc.tile_pool(name="flow", bufs=4))
-        waiting = stack.enter_context(tc.tile_pool(name="waiting", bufs=6))
+        xin = stack.enter_context(tc.tile_pool(name="xin", bufs=4))
+        flow = stack.enter_context(tc.tile_pool(name="flow", bufs=3))
+        values = stack.enter_context(tc.tile_pool(name="values", bufs=6))
         ps_view = stack.enter_context(tc.psum_pool(name="ps_view", bufs=2))
-        ps_v = stack.enter_context(tc.psum_pool(name="ps_v", bufs=1))
-        ps_mix = stack.enter_context(tc.psum_pool(name="ps_mix", bufs=1))
-        ps_y = stack.enter_context(tc.psum_pool(name="ps_y", bufs=2))
+        ps_proj = stack.enter_context(tc.psum_pool(name="ps_proj", bufs=2))
+        ps_mix = stack.enter_context(tc.psum_pool(name="ps_mix", bufs=2))
         ps_turn = stack.enter_context(tc.psum_pool(name="ps_turn", bufs=2))
 
-        ident_f32 = keep.tile([P, P], F32, name="ident_f32")
-        make_identity(nc, ident_f32[:])
+        raw_scores = keep.tile([P, NV, S], BF16, name="raw_scores")
+        for h in range(H):
+            nc.sync.dma_start(
+                out=raw_scores[h * B * NV : (h + 1) * B * NV, :, :],
+                in_=scores[:, :, :, h, :].rearrange("b i j s -> (b i) j s"),
+            )
+        x_in = {}
+
+        def load_x(b, o):
+            x_oct = xin.tile([P, OCT * D], BF16, name="x_oct")
+            nc.sync.dma_start(
+                out=x_oct[:],
+                in_=x_tiles[b, :, o * OCT : (o + 1) * OCT, :].rearrange("p r d -> p (r d)"),
+            )
+            x_in[(b, o)] = x_oct
+
+        load_x(0, 0)
+        wv_raw = keep.tile([P, PACK, D], BF16, name="w_raw")
+        nc.scalar.dma_start(out=wv_raw[:], in_=Wv.rearrange("(p a) c -> p a c", a=PACK))
+        load_x(0, V_OCT)
+        bv_raw = keep.tile([P, D], BF16, name="bv_raw")
+        nc.scalar.dma_start(out=bv_raw[:], in_=bv.partition_broadcast(P))
+        bo_all = keep.tile([P, D], BF16, name="bo_all")
+        nc.scalar.dma_start(out=bo_all[:], in_=bo.partition_broadcast(P))
+
+        ident = keep.tile([P, P], F32, name="ident")
+        make_identity(nc, ident[:])
         same_t_once = keep.tile([P, T], F32, name="same_t_once")
         nc.vector.tensor_reduce(
             out=same_t_once[:],
-            in_=ident_f32[:].rearrange("p (j t) -> p t j", j=NV, t=T),
+            in_=ident[:].rearrange("p (j t) -> p t j", j=NV, t=T),
             axis=mybir.AxisListType.X,
             op=ALU.add,
         )
         same_t = keep.tile([P, T, NV], F32, name="same_t")
         nc.vector.tensor_copy(out=same_t[:], in_=same_t_once[:].unsqueeze(2).to_broadcast([P, T, NV]))
 
-        octet_order = [o + k for k in range(TENSOR_OCTS) for o in (0, TENSOR_OCTS)]
-        x_order = [(b, o) for b in range(B) for k in range(TENSOR_OCTS) for o in (TENSOR_OCTS + k, k)]
-        x_loaded = {}
-        x_mx = {}
+        exps = {}
 
-        def load_x(n):
-            b, o = x_order[n]
-            x_oct = two.tile([P, OCT * D], BF16, name="x_oct")
-            nc.sync.dma_start(
-                out=x_oct[:],
-                in_=x_tiles[b, :, o * OCT : (o + 1) * OCT, :].rearrange("p r d -> p (r d)"),
+        def exponentials(o):
+            part = raw_scores[:].rearrange("p j (t o r) -> p o j t r", t=T, o=N_OCT, r=OCT)[:, o, :, :, :]
+            top = soft.tile([P, NV // 2, T, OCT], BF16, name="top")
+            nc.vector.tensor_max(out=top[:], in0=part[:, 0:4, :, :], in1=part[:, 4:8, :, :])
+            nc.vector.tensor_max(out=top[:, 0:2, :, :], in0=top[:, 0:2, :, :], in1=top[:, 2:4, :, :])
+            nc.vector.tensor_max(out=top[:, 0:1, :, :], in0=top[:, 0:1, :, :], in1=top[:, 1:2, :, :])
+            e = soft.tile([P, NV, T, OCT], F32, name="e")
+            nc.vector.tensor_tensor(
+                out=e[:], in0=part, in1=top[:, 0:1, :, :].to_broadcast([P, NV, T, OCT]), op=ALU.subtract
             )
-            x_loaded[n] = x_oct
-
-        def prepare_x(n):
-            b, o = x_order[n]
-            x_words = x_loaded[n][:].bitcast(F32)
-            xg = keep.tile([P, OCT * P * PACK], BF16, name="xg", align_bytes=64)
-            xg_words = xg[:].bitcast(F32)
-            by_tile = xg_words.rearrange("p (r n u) -> p r n u", r=OCT, n=P, u=2)
-            by_view = xg_words.rearrange("p (j r t u) -> p j r t u", j=NV, r=OCT, t=T, u=2)
-            for r0 in range(0, OCT, 2):
-                xt = ps_turn.tile([P, 2, 2, P], F32, tag="turn", name="xt")
-                for k in range(2):
-                    for u in range(2):
-                        first = (r0 + k) * (D // 2)
-                        nc.tensor.transpose(
-                            out=xt[:, k, u, :],
-                            in_=x_words[:, first + u : first + D // 2 : 2],
-                            identity=ident_f32[:],
-                        )
-                if o >= TENSOR_OCTS:
-                    for k in range(2):
-                        nc.scalar.copy(
-                            out=by_view[:, :, r0 + k, :, :],
-                            in_=xt[:, k, :, :].rearrange("p u (j t) -> p j t u", j=NV, t=T),
-                        )
-                else:
-                    nc.scalar.copy(
-                        out=by_tile[:, r0 : r0 + 2, :, :], in_=xt[:].rearrange("p k u n -> p k n u")
-                    )
-            kind = "view" if o >= TENSOR_OCTS else "tile"
-            codes = two.tile([P, OCT * P], U32, name="x_codes_" + kind, align_bytes=64)
-            scales = two.tile([P, OCT * P], U8, name="x_scales_" + kind, align_bytes=64)
-            nc.vector.quantize_mx(out=codes[:].bitcast(FP8X4), scales=scales[:], in_=xg[:])
-            x_mx[(b, o)] = (codes, scales)
-            if n + 2 < len(x_order):
-                load_x(n + 2)
-
-        def load_wv(raw):
-            nc.scalar.dma_start(out=raw[:], in_=Wv.rearrange("(p a) c -> p a c", a=PACK))
-
-        def load_wo(raw):
-            nc.scalar.dma_start(out=raw[:], in_=Wo.rearrange("(p a) c -> p a c", a=PACK))
+            nc.scalar.activation(out=e[:], in_=e[:], func=ACT.Exp)
+            exps[o] = e
 
         w_rows = keep.tile([P, TENSOR_TILES, P], F32, name="w_rows")
-        w_cols = keep.tile([P, VECTOR_OCTS, NV, P], F32, name="w_cols")
+        w_cols = keep.tile([P, NV, P], F32, name="w_cols")
         w_by_scene = w_rows[:].rearrange("p g (h b i) -> p b g h i", h=H, b=B, i=NV)
 
-        def spread_weights(o, e):
-            if o >= TENSOR_OCTS:
-                w = softmax_weights(nc, soft, e, "j r t", [NV, OCT, T])
-                turned = w_cols[:, o - TENSOR_OCTS, :, :]
+        def weights(o):
+            e = exps[o]
+            total = soft.tile([P, NV // 2, T, OCT], F32, name="total")
+            nc.vector.tensor_add(out=total[:], in0=e[:, 0:4, :, :], in1=e[:, 4:8, :, :])
+            nc.vector.tensor_add(out=total[:, 0:2, :, :], in0=total[:, 0:2, :, :], in1=total[:, 2:4, :, :])
+            nc.vector.tensor_add(out=total[:, 0:1, :, :], in0=total[:, 0:1, :, :], in1=total[:, 1:2, :, :])
+            nc.vector.reciprocal(out=total[:, 0:1, :, :], in_=total[:, 0:1, :, :])
+            if o == V_OCT:
+                order, shape, turned = "j r t", [P, NV, OCT, T], w_cols[:]
             else:
-                w = softmax_weights(nc, soft, e, "r j t", [OCT, NV, T])
-                turned = w_rows[:, o * OCT : (o + 1) * OCT, :]
+                order, shape, turned = "r j t", [P, OCT, NV, T], w_rows[:, o * OCT : (o + 1) * OCT, :]
+            w = soft.tile(shape, F32, name="w")
+            nc.vector.tensor_tensor(
+                out=w[:],
+                in0=e[:].rearrange("p j t r -> p " + order),
+                in1=total[:, 0:1, :, :].rearrange("p j t r -> p " + order).to_broadcast(shape),
+                op=ALU.mult,
+            )
             for first in range(0, OCT, 4):
                 wt = ps_turn.tile([P, 4, P], F32, tag="turn", name="wt")
                 for k in range(4):
                     nc.tensor.transpose(
                         out=wt[:, k, :],
                         in_=w[:, first + k, :, :].rearrange("p m n -> p (m n)"),
-                        identity=ident_f32[:],
+                        identity=ident[:],
                     )
                 nc.scalar.copy(out=turned[:, first : first + 4, :], in_=wt[:])
 
-        mixers = stack.enter_context(tc.tile_pool(name="mixers", bufs=LEAD + 2))
-        mixer_of = {}
+        x_mx = {}
+        view_xg = {}
 
-        def stage_mixers(n):
-            b, g = divmod(n, TENSOR_TILES)
-            mixer = mixers.tile([P, H, T, NV], F32, name="mixer")
-            nc.gpsimd.tensor_tensor(
-                out=mixer[:],
-                in0=w_by_scene[:, b, g, :, :].unsqueeze(2).to_broadcast([P, H, T, NV]),
-                in1=same_t[:].unsqueeze(1).to_broadcast([P, H, T, NV]),
-                op=ALU.mult,
+        def turn_x(b, o, r0):
+            words = x_in[(b, o)][:].bitcast(F32)
+            xt = ps_turn.tile([P, PAIR, 2, P], F32, tag="turn", name="xt")
+            for k in range(PAIR):
+                for u in range(2):
+                    first = (r0 + k) * WORDS
+                    nc.tensor.transpose(
+                        out=xt[:, k, u, :], in_=words[:, first + u : first + WORDS : 2], identity=ident[:]
+                    )
+            return xt
+
+        def prepare_pair(n):
+            b, q = divmod(n, PAIRS)
+            xt = turn_x(b, q // OCT_PAIRS, q % OCT_PAIRS * PAIR)
+            xg = flow.tile([P, PAIR * P * PACK], BF16, name="xg", align_bytes=64)
+            nc.scalar.copy(
+                out=xg[:].bitcast(F32).rearrange("p (k n u) -> p k n u", k=PAIR, n=P, u=2),
+                in_=xt[:].rearrange("p k u n -> p k n u"),
             )
-            mixer_of[n] = mixer
+            codes = flow.tile([P, PAIR * P], U32, name="x_codes", align_bytes=64)
+            scales = flow.tile([P, PAIR * P], U8, name="x_scales", align_bytes=64)
+            nc.vector.quantize_mx(out=codes[:].bitcast(FP8X4), scales=scales[:], in_=xg[:])
+            x_mx[n] = (codes, scales)
+
+        def prepare_views(b, r0):
+            if r0 == 0:
+                view_xg[b] = keep.tile([P, OCT * P * PACK], BF16, name="view_xg", align_bytes=64)
+            by_view = view_xg[b][:].bitcast(F32).rearrange("p (j r t u) -> p j r t u", j=NV, r=OCT, t=T, u=2)
+            xt = turn_x(b, V_OCT, r0)
+            for k in range(PAIR):
+                nc.scalar.copy(
+                    out=by_view[:, :, r0 + k, :, :],
+                    in_=xt[:, k, :, :].rearrange("p u (j t) -> p j t u", j=NV, t=T),
+                )
+            if r0 + PAIR == OCT:
+                codes = keep.tile([P, OCT * P], U32, name="view_codes", align_bytes=64)
+                scales = keep.tile([P, OCT * P], U8, name="view_scales", align_bytes=64)
+                nc.vector.quantize_mx(out=codes[:].bitcast(FP8X4), scales=scales[:], in_=view_xg[b][:])
+                x_mx[("view", b)] = (codes, scales)
 
         def project(pool, operand, first, weight):
             codes, scales = operand
@@ -221,78 +201,78 @@ def tile_crossviewattention_pa_t_kernel(tc, x, scores, Wv, bv, Wo, bo, out):
             )
             return sums
 
-        n_tiles = B * TENSOR_TILES
+        mixers = {}
         v_of = {}
         mixed_of = {}
-        grouped_of = {}
         m_mx_of = {}
-        y_sb_of = {}
+
+        def stage_mixers(n):
+            b, q = divmod(n, PAIRS)
+            for k in range(PAIR):
+                mixer = values.tile([P, H, T, NV], F32, name="mixer")
+                nc.gpsimd.tensor_tensor(
+                    out=mixer[:],
+                    in0=w_by_scene[:, b, q * PAIR + k, :, :].unsqueeze(2).to_broadcast([P, H, T, NV]),
+                    in1=same_t[:].unsqueeze(1).to_broadcast([P, H, T, NV]),
+                    op=ALU.mult,
+                )
+                mixers[(n, k)] = mixer
 
         def stage_v(n):
-            b, g = divmod(n, TENSOR_TILES)
-            v = project(ps_v, x_mx[(b, g // OCT)], (g % OCT) * P, wv_mx)
-            v_sb = flow.tile([P, D], F32, name="v_sb")
-            nc.scalar.copy(out=v_sb[:], in_=v[:])
-            nc.gpsimd.tensor_tensor(out=v_sb[:], in0=v_sb[:], in1=bv_all[:], op=ALU.add)
-            v_of[n] = v_sb
+            for k in range(PAIR):
+                v = project(ps_proj, x_mx[n], k * P, wv_mx)
+                v_sb = values.tile([P, D], F32, name="v_sb")
+                if k == 0:
+                    nc.scalar.copy(out=v_sb[:], in_=v[:])
+                    nc.gpsimd.tensor_tensor(out=v_sb[:], in0=v_sb[:], in1=bv_all[:], op=ALU.add)
+                else:
+                    nc.vector.tensor_tensor(out=v_sb[:], in0=v[:], in1=bv_all[:], op=ALU.add)
+                v_of[(n, k)] = v_sb
 
         def stage_mix(n):
-            mix = ps_mix.tile([P, D], F32, name="mix")
-            for h in range(H):
-                head = slice(h * HD, (h + 1) * HD)
-                nc.tensor.matmul(
-                    out=mix[:, head],
-                    lhsT=mixer_of[n][:, h, :, :].rearrange("p t i -> p (t i)"),
-                    rhs=v_of[n][:, head],
-                    start=True,
-                    stop=True,
-                )
-            mixed = flow.tile([P, D], BF16, name="mixed")
-            nc.scalar.copy(out=mixed[:], in_=mix[:])
+            mixed = flow.tile([P, PAIR * D], BF16, name="mixed")
+            for k in range(PAIR):
+                mix = ps_mix.tile([P, D], F32, name="mix")
+                for h in range(H):
+                    nc.tensor.matmul(
+                        out=by_head(mix[:])[:, h, :, :],
+                        lhsT=mixers[(n, k)][:, h, :, :].rearrange("p t i -> p (t i)"),
+                        rhs=by_head(v_of[(n, k)][:])[:, h, :, :],
+                        start=True,
+                        stop=True,
+                    )
+                nc.scalar.copy(out=mixed[:, k * D : (k + 1) * D], in_=mix[:])
             mixed_of[n] = mixed
 
-        def turn(mixed_rows):
-            words = mixed_rows.bitcast(F32)
-            mt = ps_turn.tile([P, 2, P], F32, tag="turn", name="mt")
+        def turn_mixed(words, mt):
             for u in range(2):
-                nc.tensor.transpose(out=mt[:, u, :], in_=words[:, u : D // 2 : 2], identity=ident_f32[:])
-            return mt
+                nc.tensor.transpose(out=mt[:, u, :], in_=words[:, u * P : (u + 1) * P], identity=ident[:])
 
         def stage_turn(n):
-            mt = turn(mixed_of[n][:])
-            grouped = waiting.tile([P, P * PACK], BF16, name="grouped", align_bytes=64)
-            nc.scalar.copy(
-                out=grouped[:].bitcast(F32).rearrange("p (i t u) -> p i t u", i=NV, t=T, u=2),
-                in_=mt[:].rearrange("p u (t i) -> p i t u", t=T, i=NV),
-            )
-            grouped_of[n] = grouped
-
-        def stage_quantise(n):
-            codes = flow.tile([P, P], U32, name="m_codes", align_bytes=64)
-            scales = flow.tile([P, P], U8, name="m_scales", align_bytes=64)
-            nc.vector.quantize_mx(
-                out=codes[:].bitcast(FP8X4),
-                scales=scales[:],
-                in_=grouped_of[n][:],
-            )
+            words = mixed_of[n][:].bitcast(F32)
+            mt = ps_turn.tile([P, PAIR, 2, P], F32, tag="turn", name="mt")
+            grouped = flow.tile([P, PAIR * P * PACK], BF16, name="grouped", align_bytes=64)
+            for k in range(PAIR):
+                turn_mixed(words[:, k * WORDS : (k + 1) * WORDS], mt[:, k, :, :])
+            for k in range(PAIR):
+                nc.scalar.copy(
+                    out=grouped[:].bitcast(F32).rearrange("p (k i t u) -> p k i t u", k=PAIR, i=NV, t=T, u=2)[
+                        :, k, :, :, :
+                    ],
+                    in_=mt[:, k, :, :].rearrange("p u (t i) -> p i t u", t=T, i=NV),
+                )
+            codes = flow.tile([P, PAIR * P], U32, name="m_codes", align_bytes=64)
+            scales = flow.tile([P, PAIR * P], U8, name="m_scales", align_bytes=64)
+            nc.vector.quantize_mx(out=codes[:].bitcast(FP8X4), scales=scales[:], in_=grouped[:])
             m_mx_of[n] = (codes, scales)
 
-        def finish_tile(b, g, operand, first):
-            y = project(ps_y, operand, first, wo_mx)
-            if g % STORE == 0:
-                y_sb_of[(b, g // STORE)] = flow.tile([P, STORE, D], F32, name="y_sb")
-            y_sb = y_sb_of[(b, g // STORE)][:, g % STORE, :]
-            if g < TENSOR_TILES:
-                nc.scalar.copy(out=y_sb, in_=y[:])
-                nc.gpsimd.tensor_tensor(out=y_sb, in0=y_sb, in1=bo_all[:], op=ALU.add)
-            else:
-                nc.vector.tensor_tensor(out=y_sb, in0=y[:], in1=bo_all[:], op=ALU.add)
-            if g % STORE == STORE - 1:
-                nc.sync.dma_start(
-                    out=out_tiles[b, :, g - STORE + 1 : g + 1, :], in_=y_sb_of[(b, g // STORE)][:]
-                )
+        def finish_pair(b, g, operand, first):
+            y_sb = flow.tile([P, PAIR, D], F32, name="y_sb")
+            for k in range(PAIR):
+                y = project(ps_proj, operand, first + k * P, wo_mx)
+                nc.vector.tensor_tensor(out=y_sb[:, k, :], in0=y[:], in1=bo_all[:], op=ALU.add)
+            nc.sync.dma_start(out=out_tiles[b, :, g : g + PAIR, :], in_=y_sb[:])
 
-        n_pairs = B * VECTOR_OCTS * NV
         view_sums = {}
         octet_sums = {}
         octet_mixed = {}
@@ -300,107 +280,126 @@ def tile_crossviewattention_pa_t_kernel(tc, x, scores, Wv, bv, Wo, bo, out):
         octet_mx = {}
 
         def project_view(k):
-            m, j = divmod(k, NV)
-            octet = (m // VECTOR_OCTS, TENSOR_OCTS + m % VECTOR_OCTS)
-            view_sums[k] = project(ps_view, x_mx[octet], j * P, wv_mx)
+            b, j = divmod(k, NV)
+            view_sums[k] = project(ps_view, x_mx[("view", b)], j * P, wv_mx)
 
-        def add_view(k):
-            m, j = divmod(k, NV)
-            b = m // VECTOR_OCTS
-            if j == 0:
-                octet_sums[m] = keep.tile([P, NV, D], F32, name="acc")
-            if j == NV - 1:
-                octet_mixed[m] = keep.tile([P, NV, D], BF16, name="mixed_v")
-            acc = octet_sums[m]
-            for i in range(NV):
-                for h in range(H):
-                    head = slice(h * HD, (h + 1) * HD)
-                    col = (h * B + b) * NV + i
-                    before = bv_all[:, head] if j == 0 else acc[:, i, head]
-                    after = octet_mixed[m][:, i, head] if j == NV - 1 else acc[:, i, head]
-                    nc.vector.scalar_tensor_tensor(
-                        out=after,
-                        in0=view_sums[k][:, head],
-                        scalar=w_cols[:, m % VECTOR_OCTS, j, col : col + 1],
-                        in1=before,
-                        op0=ALU.mult,
-                        op1=ALU.add,
-                    )
+        def add_unit(n):
+            k, i = divmod(n, NV)
+            b, j = divmod(k, NV)
+            if n % (NV * NV) == 0:
+                octet_sums[b] = keep.tile([P, NV, D], F32, name="acc")
+            if i == 0 and j == NV - 1:
+                octet_mixed[b] = keep.tile([P, NV * D], BF16, name="mixed_v")
+            if i == 0 and k + 1 < B * NV and ("view", (k + 1) // NV) in x_mx:
+                project_view(k + 1)
+            before = bv_all[:] if j == 0 else octet_sums[b][:, i, :]
+            after = octet_mixed[b][:, i * D : (i + 1) * D] if j == NV - 1 else octet_sums[b][:, i, :]
+            for h in range(H):
+                col = (h * B + b) * NV + i
+                nc.vector.scalar_tensor_tensor(
+                    out=by_head(after)[:, h, :, :],
+                    in0=by_head(view_sums[k][:])[:, h, :, :],
+                    scalar=w_cols[:, j, col : col + 1],
+                    in1=by_head(before)[:, h, :, :],
+                    op0=ALU.mult,
+                    op1=ALU.add,
+                )
 
-        def turn_query_view(m, i):
+        def turn_query_view(b, i):
             if i == 0:
-                octet_grouped[m] = keep.tile([P, OCT * P * PACK], BF16, name="mgv", align_bytes=64)
-            mt = turn(octet_mixed[m][:, i, :])
-            by_tile = octet_grouped[m][:].bitcast(F32).rearrange(
+                octet_grouped[b] = keep.tile([P, OCT * P * PACK], BF16, name="mgv", align_bytes=64)
+            mt = ps_turn.tile([P, 2, P], F32, tag="turn", name="mtv")
+            turn_mixed(octet_mixed[b][:].bitcast(F32)[:, i * WORDS : (i + 1) * WORDS], mt[:])
+            by_tile = octet_grouped[b][:].bitcast(F32).rearrange(
                 "p (r i t u) -> p r i t u", r=OCT, i=NV, t=T, u=2
             )
             nc.scalar.copy(
                 out=by_tile[:, :, i, :, :], in_=mt[:].rearrange("p u (r t) -> p r t u", r=OCT, t=T)
             )
 
-        def quantise_octet(m):
+        def quantise_octet(b):
             codes = keep.tile([P, OCT * P], U32, name="mv_codes", align_bytes=64)
             scales = keep.tile([P, OCT * P], U8, name="mv_scales", align_bytes=64)
+            nc.vector.quantize_mx(out=codes[:].bitcast(FP8X4), scales=scales[:], in_=octet_grouped[b][:])
+            octet_mx[b] = (codes, scales)
+
+        def quantise_weight(name, raw, permute):
+            grouped = keep.tile([P, D, PACK], BF16, name="w_grouped", align_bytes=64)
+            if permute:
+                for u in range(2):
+                    nc.vector.tensor_copy(
+                        out=grouped[:].rearrange("p (u q e) a -> p u q e a", u=2, e=2)[:, u, :, :, :],
+                        in_=raw[:].rearrange("p a (q u e) -> p u q e a", u=2, e=2)[:, u, :, :, :],
+                    )
+            else:
+                nc.vector.tensor_copy(out=grouped[:], in_=raw[:].rearrange("p a c -> p c a"))
+            codes = keep.tile([P, D], U32, name=name + "_codes", align_bytes=64)
+            scales = keep.tile([P, D], U8, name=name + "_scales", align_bytes=64)
             nc.vector.quantize_mx(
-                out=codes[:].bitcast(FP8X4),
-                scales=scales[:],
-                in_=octet_grouped[m][:],
+                out=codes[:].bitcast(FP8X4), scales=scales[:], in_=grouped[:].rearrange("p c a -> p (c a)")
             )
-            octet_mx[m] = (codes, scales)
+            return codes, scales
 
-        raw_scores = load_scores(nc, setup, scores)
-        load_x(0)
-        load_x(1)
-        wv_mx = quantise_weight(nc, setup, keep, "wv", load_wv)
+        exponentials(0)
+        wv_mx = quantise_weight("wv", wv_raw, True)
         bv_all = keep.tile([P, D], BF16, name="bv_all")
-        nc.scalar.dma_start(out=bv_all[:], in_=bv.partition_broadcast(P))
-        bo_all = keep.tile([P, D], BF16, name="bo_all")
-        nc.scalar.dma_start(out=bo_all[:], in_=bo.partition_broadcast(P))
-        prepare_x(0)
-        exps = {}
-        for k in range(N_OCT + 1):
-            if k < N_OCT:
-                exps[k] = softmax_exponentials(nc, soft, raw_scores, octet_order[k])
-            if k > 0:
-                spread_weights(octet_order[k - 1], exps[k - 1])
-            if k == 1:
-                for n in range(LEAD):
-                    stage_mixers(n)
-                prepare_x(1)
-        wo_mx = quantise_weight(nc, setup, keep, "wo", load_wo)
+        nc.vector.tensor_copy(
+            out=bv_all[:].rearrange("p (u q e) -> p u q e", u=2, e=2),
+            in_=bv_raw[:].rearrange("p (q u e) -> p u q e", u=2, e=2),
+        )
+        prepare_pair(0)
+        weights(0)
+        for n in range(LEAD):
+            stage_mixers(n)
+        exponentials(V_OCT)
+        stage_v(0)
+        prepare_pair(1)
+        for r0 in range(0, OCT, PAIR):
+            prepare_views(0, r0)
+        weights(V_OCT)
         project_view(0)
-        project_view(1)
-        add_view(0)
+        load_x(0, 1)
+        load_x(0, 2)
+        wo_raw = keep.tile([P, PACK, D], BF16, name="w_raw")
+        nc.scalar.dma_start(out=wo_raw[:], in_=Wo.rearrange("(p a) c -> p a c", a=PACK))
+        wo_mx = quantise_weight("wo", wo_raw, False)
 
-        for count in range(n_pairs + NV - 1):
-            s = count - 1
-            if 0 <= s - 4 < n_tiles:
-                finish_tile((s - 4) // TENSOR_TILES, (s - 4) % TENSOR_TILES, m_mx_of[s - 4], 0)
-            if 0 <= s + 1 < n_tiles:
-                stage_v(s + 1)
-            if 0 <= s - 3 < n_tiles:
-                stage_quantise(s - 3)
-            if LEAD <= s + LEAD < n_tiles:
-                stage_mixers(s + LEAD)
-            if 0 <= s < n_tiles:
-                stage_mix(s)
-            if count + 2 < n_pairs:
-                project_view(count + 2)
-            since = [count - (NV * m + NV - 1) for m in range(B * VECTOR_OCTS)]
-            for m in range(B * VECTOR_OCTS):
-                if since[m] == NV // 2:
-                    quantise_octet(m)
-            if count + 1 < n_pairs:
-                add_view(count + 1)
-            if 0 <= s - 1 < n_tiles:
+        n_steps = N_PAIRS + 2
+        for s in range(n_steps):
+            if s + 2 < N_PAIRS:
+                prepare_pair(s + 2)
+            if 6 <= s < 10:
+                prepare_views(1, (s - 6) * PAIR)
+            if 0 <= s - 1 < N_PAIRS:
                 stage_turn(s - 1)
-            for m in range(B * VECTOR_OCTS):
-                for k in range(2):
-                    if 0 <= since[m] < NV // 2:
-                        turn_query_view(m, 2 * since[m] + k)
-                    if NV // 2 <= since[m] < NV:
-                        r = 2 * (since[m] - NV // 2) + k
-                        g = (TENSOR_OCTS + m % VECTOR_OCTS) * OCT + r
-                        finish_tile(m // VECTOR_OCTS, g, octet_mx[m], r * P)
-            if count % 4 == 1 and 2 + count // 4 < len(x_order):
-                prepare_x(2 + count // 4)
+            if s == 1:
+                load_x(1, 0)
+                load_x(1, V_OCT)
+            if s == 6:
+                load_x(1, 1)
+            if s == 10:
+                load_x(1, 2)
+            if s + 1 < N_PAIRS:
+                stage_v(s + 1)
+            if 0 <= s - 2 < N_PAIRS:
+                n = s - 2
+                finish_pair(n // PAIRS, n % PAIRS * PAIR, m_mx_of[n], 0)
+            if s + LEAD < N_PAIRS:
+                stage_mixers(s + LEAD)
+            if s < N_PAIRS:
+                stage_mix(s)
+            if s == 0 or s == 3:
+                o = 1 if s == 0 else 2
+                exponentials(o)
+                weights(o)
+            for n in range(s * UNITS, min((s + 1) * UNITS, N_UNITS)):
+                add_unit(n)
+            for b, done in ((0, 11), (1, 22)):
+                if done <= s < done + 2:
+                    for i in range((s - done) * 4, (s - done) * 4 + 4):
+                        turn_query_view(b, i)
+                if s == done + 1:
+                    quantise_octet(b)
+                if done + 2 <= s < done + 4:
+                    for r in range((s - done - 2) * 4, (s - done - 2) * 4 + 4, PAIR):
+                        finish_pair(b, V_OCT * OCT + r, octet_mx[b], r * P)

@@ -85,15 +85,13 @@ def tile_crossviewattention_pa_t_kernel(tc, x, scores, Wv, bv, Wo, bo, out):
 
         ident = keep.tile([P, P], F32, name="ident")
         make_identity(nc, ident[:])
-        same_t_once = keep.tile([P, T], F32, name="same_t_once")
+        same_t = keep.tile([P, T], F32, name="same_t")
         nc.vector.tensor_reduce(
-            out=same_t_once[:],
+            out=same_t[:],
             in_=ident[:].rearrange("p (j t) -> p t j", j=NV, t=T),
             axis=mybir.AxisListType.X,
             op=ALU.add,
         )
-        same_t = keep.tile([P, T, NV], F32, name="same_t")
-        nc.vector.tensor_copy(out=same_t[:], in_=same_t_once[:].unsqueeze(2).to_broadcast([P, T, NV]))
 
         exps = {}
 
@@ -112,7 +110,7 @@ def tile_crossviewattention_pa_t_kernel(tc, x, scores, Wv, bv, Wo, bo, out):
 
         w_rows = keep.tile([P, TENSOR_TILES, P], F32, name="w_rows")
         w_cols = keep.tile([P, NV, P], F32, name="w_cols")
-        w_by_scene = w_rows[:].rearrange("p g (h b i) -> p b g h i", h=H, b=B, i=NV)
+        w_by_scene = w_rows[:].rearrange("p g (h b i) -> p b (g h) i", h=H, b=B, i=NV)
 
         def weights(o):
             e = exps[o]
@@ -208,25 +206,22 @@ def tile_crossviewattention_pa_t_kernel(tc, x, scores, Wv, bv, Wo, bo, out):
 
         def stage_mixers(n):
             b, q = divmod(n, PAIRS)
-            for k in range(PAIR):
-                mixer = values.tile([P, H, T, NV], F32, name="mixer")
-                nc.gpsimd.tensor_tensor(
-                    out=mixer[:],
-                    in0=w_by_scene[:, b, q * PAIR + k, :, :].unsqueeze(2).to_broadcast([P, H, T, NV]),
-                    in1=same_t[:].unsqueeze(1).to_broadcast([P, H, T, NV]),
-                    op=ALU.mult,
+            w = w_by_scene[:, b, q * PAIR * H : (q + 1) * PAIR * H, :]
+            mixer = flow.tile([P, PAIR * H, T, NV], F32, name="mixer")
+            for t in range(T):
+                nc.scalar.activation(
+                    out=mixer[:, :, t, :],
+                    in_=w,
+                    func=ACT.Copy,
+                    scale=same_t[:, t : t + 1],
                 )
-                mixers[(n, k)] = mixer
+            mixers[n] = mixer
 
         def stage_v(n):
             for k in range(PAIR):
                 v = project(ps_proj, x_mx[n], k * P, wv_mx)
                 v_sb = values.tile([P, D], F32, name="v_sb")
-                if k == 0:
-                    nc.scalar.copy(out=v_sb[:], in_=v[:])
-                    nc.gpsimd.tensor_tensor(out=v_sb[:], in0=v_sb[:], in1=bv_all[:], op=ALU.add)
-                else:
-                    nc.vector.tensor_tensor(out=v_sb[:], in0=v[:], in1=bv_all[:], op=ALU.add)
+                nc.vector.tensor_tensor(out=v_sb[:], in0=v[:], in1=bv_all[:], op=ALU.add)
                 v_of[(n, k)] = v_sb
 
         def stage_mix(n):
@@ -236,7 +231,7 @@ def tile_crossviewattention_pa_t_kernel(tc, x, scores, Wv, bv, Wo, bo, out):
                 for h in range(H):
                     nc.tensor.matmul(
                         out=by_head(mix[:])[:, h, :, :],
-                        lhsT=mixers[(n, k)][:, h, :, :].rearrange("p t i -> p (t i)"),
+                        lhsT=mixers[n][:, k * H + h, :, :].rearrange("p t i -> p (t i)"),
                         rhs=by_head(v_of[(n, k)][:])[:, h, :, :],
                         start=True,
                         stop=True,

@@ -265,7 +265,11 @@ def tile_crossviewattention_pa_t_kernel(tc, x, scores, Wv, bv, Wo, bo, out):
             y_sb = flow.tile([P, PAIR, D], F32, name="y_sb")
             for k in range(PAIR):
                 y = project(ps_proj, operand, first + k * P, wo_mx)
-                nc.vector.tensor_tensor(out=y_sb[:, k, :], in0=y[:], in1=bo_all[:], op=ALU.add)
+                if k == 0 and g < TENSOR_TILES:
+                    nc.scalar.copy(out=y_sb[:, k, :], in_=y[:])
+                    nc.gpsimd.tensor_tensor(out=y_sb[:, k, :], in0=y_sb[:, k, :], in1=bo_all[:], op=ALU.add)
+                else:
+                    nc.vector.tensor_tensor(out=y_sb[:, k, :], in0=y[:], in1=bo_all[:], op=ALU.add)
             nc.sync.dma_start(out=out_tiles[b, :, g : g + PAIR, :], in_=y_sb[:])
 
         view_sums = {}

@@ -221,7 +221,8 @@ def tile_crossviewattention_pa_t_kernel(tc, x, scores, Wv, bv, Wo, bo, out):
             for k in range(PAIR):
                 v = project(ps_proj, x_mx[n], k * P, wv_mx)
                 v_sb = values.tile([P, D], F32, name="v_sb")
-                nc.vector.tensor_tensor(out=v_sb[:], in0=v[:], in1=bv_all[:], op=ALU.add)
+                nc.scalar.copy(out=v_sb[:], in_=v[:])
+                nc.gpsimd.tensor_tensor(out=v_sb[:], in0=v_sb[:], in1=bv_all[:], op=ALU.add)
                 v_of[(n, k)] = v_sb
 
         def stage_mix(n):

@@ -24,16 +24,16 @@ T = P // NV
 G = S // T
 OCT = 8
 N_OCT = G // OCT
-TENSOR_OCTS = 3
-TENSOR_TILES = TENSOR_OCTS * OCT
-V_OCT = N_OCT - 1
+T_OCTS = [(0, 0), (0, 1), (1, 0), (1, 1), (1, 2)]
+V_OCTS = [(0, 3), (0, 2), (1, 3)]
+ROW_OCTS = 3
 PAIR = 2
-PAIRS = TENSOR_TILES // PAIR
-N_PAIRS = B * PAIRS
 OCT_PAIRS = OCT // PAIR
+N_PAIRS = len(T_OCTS) * OCT_PAIRS
 LEAD = 2
-UNITS = 6
-N_UNITS = B * NV * NV
+UNITS = 11
+OCT_UNITS = NV * NV
+N_UNITS = len(V_OCTS) * OCT_UNITS
 
 FLOPS = 2 * 2 * B * NV * S * D * D + 2 * B * NV * NV * S * D
 
@@ -77,7 +77,7 @@ def tile_crossviewattention_pa_t_kernel(tc, x, scores, Wv, bv, Wo, bo, out):
         load_x(0, 0)
         wv_raw = keep.tile([P, PACK, D], BF16, name="w_raw")
         nc.scalar.dma_start(out=wv_raw[:], in_=Wv.rearrange("(p a) c -> p a c", a=PACK))
-        load_x(0, V_OCT)
+        load_x(0, 3)
         bv_raw = keep.tile([P, D], BF16, name="bv_raw")
         nc.scalar.dma_start(out=bv_raw[:], in_=bv.partition_broadcast(P))
         bo_all = keep.tile([P, D], BF16, name="bo_all")
@@ -95,42 +95,44 @@ def tile_crossviewattention_pa_t_kernel(tc, x, scores, Wv, bv, Wo, bo, out):
 
         exps = {}
 
-        def exponentials(o):
-            part = raw_scores[:].rearrange("p j (t o r) -> p o j t r", t=T, o=N_OCT, r=OCT)[:, o, :, :, :]
-            top = soft.tile([P, NV // 2, T, OCT], BF16, name="top")
+        def exponentials(o, r0=0, nr=OCT):
+            part = raw_scores[:].rearrange("p j (t o r) -> p o j t r", t=T, o=N_OCT, r=OCT)[
+                :, o, :, :, r0 : r0 + nr
+            ]
+            top = soft.tile([P, NV // 2, T, nr], BF16, name="top")
             nc.vector.tensor_max(out=top[:], in0=part[:, 0:4, :, :], in1=part[:, 4:8, :, :])
             nc.vector.tensor_max(out=top[:, 0:2, :, :], in0=top[:, 0:2, :, :], in1=top[:, 2:4, :, :])
             nc.vector.tensor_max(out=top[:, 0:1, :, :], in0=top[:, 0:1, :, :], in1=top[:, 1:2, :, :])
-            e = soft.tile([P, NV, T, OCT], F32, name="e")
+            e = soft.tile([P, NV, T, nr], F32, name="e")
             nc.vector.tensor_tensor(
-                out=e[:], in0=part, in1=top[:, 0:1, :, :].to_broadcast([P, NV, T, OCT]), op=ALU.subtract
+                out=e[:], in0=part, in1=top[:, 0:1, :, :].to_broadcast([P, NV, T, nr]), op=ALU.subtract
             )
             nc.scalar.activation(out=e[:], in_=e[:], func=ACT.Exp)
-            exps[o] = e
+            exps[(o, r0)] = e
 
-        w_rows = keep.tile([P, TENSOR_TILES, P], F32, name="w_rows")
-        w_cols = keep.tile([P, NV, P], F32, name="w_cols")
+        w_rows = keep.tile([P, ROW_OCTS * OCT, P], F32, name="w_rows")
         w_by_scene = w_rows[:].rearrange("p g (h b i) -> p b (g h) i", h=H, b=B, i=NV)
+        w_cols = {}
+        totals = {}
 
-        def weights(o):
-            e = exps[o]
-            total = soft.tile([P, NV // 2, T, OCT], F32, name="total")
+        def normalise(o, r0=0, nr=OCT):
+            e = exps[(o, r0)]
+            total = soft.tile([P, NV // 2, T, nr], F32, name="total")
             nc.vector.tensor_add(out=total[:], in0=e[:, 0:4, :, :], in1=e[:, 4:8, :, :])
             nc.vector.tensor_add(out=total[:, 0:2, :, :], in0=total[:, 0:2, :, :], in1=total[:, 2:4, :, :])
             nc.vector.tensor_add(out=total[:, 0:1, :, :], in0=total[:, 0:1, :, :], in1=total[:, 1:2, :, :])
             nc.vector.reciprocal(out=total[:, 0:1, :, :], in_=total[:, 0:1, :, :])
-            if o == V_OCT:
-                order, shape, turned = "j r t", [P, NV, OCT, T], w_cols[:]
-            else:
-                order, shape, turned = "r j t", [P, OCT, NV, T], w_rows[:, o * OCT : (o + 1) * OCT, :]
+            totals[(o, r0)] = total
+
+        def weights(o, r0, order, shape, turned):
             w = soft.tile(shape, F32, name="w")
             nc.vector.tensor_tensor(
                 out=w[:],
-                in0=e[:].rearrange("p j t r -> p " + order),
-                in1=total[:, 0:1, :, :].rearrange("p j t r -> p " + order).to_broadcast(shape),
+                in0=exps[(o, r0)][:].rearrange("p j t r -> p " + order),
+                in1=totals[(o, r0)][:, 0:1, :, :].rearrange("p j t r -> p " + order).to_broadcast(shape),
                 op=ALU.mult,
             )
-            for first in range(0, OCT, 4):
+            for first in range(0, shape[1], 4):
                 wt = ps_turn.tile([P, 4, P], F32, tag="turn", name="wt")
                 for k in range(4):
                     nc.tensor.transpose(
@@ -139,6 +141,13 @@ def tile_crossviewattention_pa_t_kernel(tc, x, scores, Wv, bv, Wo, bo, out):
                         identity=ident[:],
                     )
                 nc.scalar.copy(out=turned[:, first : first + 4, :], in_=wt[:])
+
+        def row_weights(o, r0=0, nr=OCT):
+            weights(o, r0, "r j t", [P, nr, NV, T], w_rows[:, o * OCT + r0 : o * OCT + r0 + nr, :])
+
+        def col_weights(o):
+            w_cols[o] = keep.tile([P, NV, P], F32, name="w_cols_" + str(o))
+            weights(o, 0, "j r t", [P, NV, OCT, T], w_cols[o][:])
 
         x_mx = {}
         view_xg = {}
@@ -155,8 +164,8 @@ def tile_crossviewattention_pa_t_kernel(tc, x, scores, Wv, bv, Wo, bo, out):
             return xt
 
         def prepare_pair(n):
-            b, q = divmod(n, PAIRS)
-            xt = turn_x(b, q // OCT_PAIRS, q % OCT_PAIRS * PAIR)
+            b, o = T_OCTS[n // OCT_PAIRS]
+            xt = turn_x(b, o, n % OCT_PAIRS * PAIR)
             xg = flow.tile([P, PAIR * P * PACK], BF16, name="xg", align_bytes=64)
             nc.scalar.copy(
                 out=xg[:].bitcast(F32).rearrange("p (k n u) -> p k n u", k=PAIR, n=P, u=2),
@@ -167,21 +176,22 @@ def tile_crossviewattention_pa_t_kernel(tc, x, scores, Wv, bv, Wo, bo, out):
             nc.vector.quantize_mx(out=codes[:].bitcast(FP8X4), scales=scales[:], in_=xg[:])
             x_mx[n] = (codes, scales)
 
-        def prepare_views(b, r0):
+        def prepare_views(m, r0):
+            b, o = V_OCTS[m]
             if r0 == 0:
-                view_xg[b] = keep.tile([P, OCT * P * PACK], BF16, name="view_xg", align_bytes=64)
-            by_view = view_xg[b][:].bitcast(F32).rearrange("p (j r t u) -> p j r t u", j=NV, r=OCT, t=T, u=2)
-            xt = turn_x(b, V_OCT, r0)
+                view_xg[m] = keep.tile([P, OCT * P * PACK], BF16, name="view_xg", align_bytes=64)
+            by_view = view_xg[m][:].bitcast(F32).rearrange("p (j r t u) -> p j r t u", j=NV, r=OCT, t=T, u=2)
+            xt = turn_x(b, o, r0)
             for k in range(PAIR):
                 nc.scalar.copy(
                     out=by_view[:, :, r0 + k, :, :],
                     in_=xt[:, k, :, :].rearrange("p u (j t) -> p j t u", j=NV, t=T),
                 )
             if r0 + PAIR == OCT:
-                codes = keep.tile([P, OCT * P], U32, name="view_codes", align_bytes=64)
-                scales = keep.tile([P, OCT * P], U8, name="view_scales", align_bytes=64)
-                nc.vector.quantize_mx(out=codes[:].bitcast(FP8X4), scales=scales[:], in_=view_xg[b][:])
-                x_mx[("view", b)] = (codes, scales)
+                codes = soft.tile([P, OCT * P], U32, name="view_codes", align_bytes=64)
+                scales = soft.tile([P, OCT * P], U8, name="view_scales", align_bytes=64)
+                nc.vector.quantize_mx(out=codes[:].bitcast(FP8X4), scales=scales[:], in_=view_xg[m][:])
+                x_mx[("view", m)] = (codes, scales)
 
         def project(pool, operand, first, weight):
             codes, scales = operand
@@ -205,16 +215,27 @@ def tile_crossviewattention_pa_t_kernel(tc, x, scores, Wv, bv, Wo, bo, out):
         m_mx_of = {}
 
         def stage_mixers(n):
-            b, q = divmod(n, PAIRS)
-            w = w_by_scene[:, b, q * PAIR * H : (q + 1) * PAIR * H, :]
+            b, o = T_OCTS[n // OCT_PAIRS]
+            g = o * OCT + n % OCT_PAIRS * PAIR
+            w = w_by_scene[:, b, g * H : (g + PAIR) * H, :]
             mixer = flow.tile([P, PAIR * H, T, NV], F32, name="mixer")
-            for t in range(T):
-                nc.scalar.activation(
-                    out=mixer[:, :, t, :],
-                    in_=w,
-                    func=ACT.Copy,
-                    scale=same_t[:, t : t + 1],
-                )
+            if n % 2 == 0:
+                for k in range(PAIR):
+                    heads = slice(k * H, (k + 1) * H)
+                    nc.gpsimd.tensor_tensor(
+                        out=mixer[:, heads, :, :],
+                        in0=w[:, heads, :].unsqueeze(2).to_broadcast([P, H, T, NV]),
+                        in1=same_t[:].unsqueeze(1).unsqueeze(3).to_broadcast([P, H, T, NV]),
+                        op=ALU.mult,
+                    )
+            else:
+                for t in range(T):
+                    nc.scalar.activation(
+                        out=mixer[:, :, t, :],
+                        in_=w,
+                        func=ACT.Copy,
+                        scale=same_t[:, t : t + 1],
+                    )
             mixers[n] = mixer
 
         def stage_v(n):
@@ -262,11 +283,11 @@ def tile_crossviewattention_pa_t_kernel(tc, x, scores, Wv, bv, Wo, bo, out):
             nc.vector.quantize_mx(out=codes[:].bitcast(FP8X4), scales=scales[:], in_=grouped[:])
             m_mx_of[n] = (codes, scales)
 
-        def finish_pair(b, g, operand, first):
+        def finish_pair(b, g, operand, first, on_scalar):
             y_sb = flow.tile([P, PAIR, D], F32, name="y_sb")
             for k in range(PAIR):
                 y = project(ps_proj, operand, first + k * P, wo_mx)
-                if k == 0 and g < TENSOR_TILES:
+                if on_scalar:
                     nc.scalar.copy(out=y_sb[:, k, :], in_=y[:])
                     nc.gpsimd.tensor_tensor(out=y_sb[:, k, :], in0=y_sb[:, k, :], in1=bo_all[:], op=ALU.add)
                 else:
@@ -280,48 +301,49 @@ def tile_crossviewattention_pa_t_kernel(tc, x, scores, Wv, bv, Wo, bo, out):
         octet_mx = {}
 
         def project_view(k):
-            b, j = divmod(k, NV)
-            view_sums[k] = project(ps_view, x_mx[("view", b)], j * P, wv_mx)
+            m, j = divmod(k, NV)
+            view_sums[k] = project(ps_view, x_mx[("view", m)], j * P, wv_mx)
 
         def add_unit(n):
             k, i = divmod(n, NV)
-            b, j = divmod(k, NV)
-            if n % (NV * NV) == 0:
-                octet_sums[b] = keep.tile([P, NV, D], F32, name="acc")
+            m, j = divmod(k, NV)
+            b, o = V_OCTS[m]
+            if i == 0 and j == 0:
+                octet_sums[m] = keep.tile([P, NV, D], F32, name="acc")
             if i == 0 and j == NV - 1:
-                octet_mixed[b] = keep.tile([P, NV * D], BF16, name="mixed_v")
-            if i == 0 and k + 1 < B * NV and ("view", (k + 1) // NV) in x_mx:
+                octet_mixed[m] = keep.tile([P, NV * D], BF16, name="mixed_v")
+            if i == 0 and n + NV < N_UNITS:
                 project_view(k + 1)
-            before = bv_all[:] if j == 0 else octet_sums[b][:, i, :]
-            after = octet_mixed[b][:, i * D : (i + 1) * D] if j == NV - 1 else octet_sums[b][:, i, :]
+            before = bv_all[:] if j == 0 else octet_sums[m][:, i, :]
+            after = octet_mixed[m][:, i * D : (i + 1) * D] if j == NV - 1 else octet_sums[m][:, i, :]
             for h in range(H):
                 col = (h * B + b) * NV + i
                 nc.vector.scalar_tensor_tensor(
                     out=by_head(after)[:, h, :, :],
                     in0=by_head(view_sums[k][:])[:, h, :, :],
-                    scalar=w_cols[:, j, col : col + 1],
+                    scalar=w_cols[o][:, j, col : col + 1],
                     in1=by_head(before)[:, h, :, :],
                     op0=ALU.mult,
                     op1=ALU.add,
                 )
 
-        def turn_query_view(b, i):
+        def turn_query_view(m, i):
             if i == 0:
-                octet_grouped[b] = keep.tile([P, OCT * P * PACK], BF16, name="mgv", align_bytes=64)
+                octet_grouped[m] = keep.tile([P, OCT * P * PACK], BF16, name="mgv", align_bytes=64)
             mt = ps_turn.tile([P, 2, P], F32, tag="turn", name="mtv")
-            turn_mixed(octet_mixed[b][:].bitcast(F32)[:, i * WORDS : (i + 1) * WORDS], mt[:])
-            by_tile = octet_grouped[b][:].bitcast(F32).rearrange(
+            turn_mixed(octet_mixed[m][:].bitcast(F32)[:, i * WORDS : (i + 1) * WORDS], mt[:])
+            by_tile = octet_grouped[m][:].bitcast(F32).rearrange(
                 "p (r i t u) -> p r i t u", r=OCT, i=NV, t=T, u=2
             )
             nc.scalar.copy(
                 out=by_tile[:, :, i, :, :], in_=mt[:].rearrange("p u (r t) -> p r t u", r=OCT, t=T)
             )
 
-        def quantise_octet(b):
+        def quantise_octet(m):
             codes = keep.tile([P, OCT * P], U32, name="mv_codes", align_bytes=64)
             scales = keep.tile([P, OCT * P], U8, name="mv_scales", align_bytes=64)
-            nc.vector.quantize_mx(out=codes[:].bitcast(FP8X4), scales=scales[:], in_=octet_grouped[b][:])
-            octet_mx[b] = (codes, scales)
+            nc.vector.quantize_mx(out=codes[:].bitcast(FP8X4), scales=scales[:], in_=octet_grouped[m][:])
+            octet_mx[m] = (codes, scales)
 
         def quantise_weight(name, raw, permute):
             grouped = keep.tile([P, D, PACK], BF16, name="w_grouped", align_bytes=64)
@@ -340,7 +362,8 @@ def tile_crossviewattention_pa_t_kernel(tc, x, scores, Wv, bv, Wo, bo, out):
             )
             return codes, scales
 
-        exponentials(0)
+        HALF = OCT // 2
+        exponentials(0, 0, HALF)
         wv_mx = quantise_weight("wv", wv_raw, True)
         bv_all = keep.tile([P, D], BF16, name="bv_all")
         nc.vector.tensor_copy(
@@ -348,58 +371,72 @@ def tile_crossviewattention_pa_t_kernel(tc, x, scores, Wv, bv, Wo, bo, out):
             in_=bv_raw[:].rearrange("p (q u e) -> p u q e", u=2, e=2),
         )
         prepare_pair(0)
-        weights(0)
+        normalise(0, 0, HALF)
+        row_weights(0, 0, HALF)
         for n in range(LEAD):
             stage_mixers(n)
-        exponentials(V_OCT)
         stage_v(0)
+        exponentials(3)
         prepare_pair(1)
         for r0 in range(0, OCT, PAIR):
             prepare_views(0, r0)
-        weights(V_OCT)
+        normalise(3)
+        col_weights(3)
         project_view(0)
         load_x(0, 1)
         load_x(0, 2)
-        wo_raw = keep.tile([P, PACK, D], BF16, name="w_raw")
-        nc.scalar.dma_start(out=wo_raw[:], in_=Wo.rearrange("(p a) c -> p a c", a=PACK))
-        wo_mx = quantise_weight("wo", wo_raw, False)
+        exponentials(0, HALF, HALF)
+        normalise(0, HALF, HALF)
+        row_weights(0, HALF, HALF)
 
+        done = [-(-(m + 1) * OCT_UNITS // UNITS) for m in range(len(V_OCTS))]
+        view_steps = {first + k: (m, k * PAIR) for m, first in ((1, 2), (2, 7)) for k in range(OCT_PAIRS)}
         n_steps = N_PAIRS + 2
         for s in range(n_steps):
             if s + 2 < N_PAIRS:
                 prepare_pair(s + 2)
-            if 6 <= s < 10:
-                prepare_views(1, (s - 6) * PAIR)
+            if s in view_steps:
+                prepare_views(*view_steps[s])
             if 0 <= s - 1 < N_PAIRS:
                 stage_turn(s - 1)
             if s == 1:
                 load_x(1, 0)
-                load_x(1, V_OCT)
-            if s == 6:
+                load_x(1, 3)
+            if s == 5:
                 load_x(1, 1)
-            if s == 10:
                 load_x(1, 2)
             if s + 1 < N_PAIRS:
                 stage_v(s + 1)
+            if s == 0:
+                wo_raw = keep.tile([P, PACK, D], BF16, name="w_raw")
+                nc.scalar.dma_start(out=wo_raw[:], in_=Wo.rearrange("(p a) c -> p a c", a=PACK))
+                wo_mx = quantise_weight("wo", wo_raw, False)
             if 0 <= s - 2 < N_PAIRS:
                 n = s - 2
-                finish_pair(n // PAIRS, n % PAIRS * PAIR, m_mx_of[n], 0)
+                b, o = T_OCTS[n // OCT_PAIRS]
+                finish_pair(b, o * OCT + n % OCT_PAIRS * PAIR, m_mx_of[n], 0, True)
             if s + LEAD < N_PAIRS:
                 stage_mixers(s + LEAD)
             if s < N_PAIRS:
                 stage_mix(s)
-            if s == 0 or s == 3:
-                o = 1 if s == 0 else 2
-                exponentials(o)
-                weights(o)
+            if s == 0:
+                exponentials(1)
+                normalise(1)
+                row_weights(1)
+            if s == 3:
+                exponentials(2)
+                normalise(2)
+                col_weights(2)
+                row_weights(2)
             for n in range(s * UNITS, min((s + 1) * UNITS, N_UNITS)):
                 add_unit(n)
-            for b, done in ((0, 11), (1, 22)):
-                if done <= s < done + 2:
-                    for i in range((s - done) * 4, (s - done) * 4 + 4):
-                        turn_query_view(b, i)
-                if s == done + 1:
-                    quantise_octet(b)
-                if done + 2 <= s < done + 4:
-                    for r in range((s - done - 2) * 4, (s - done - 2) * 4 + 4, PAIR):
-                        finish_pair(b, V_OCT * OCT + r, octet_mx[b], r * P)
+            for m in range(len(V_OCTS)):
+                b, o = V_OCTS[m]
+                if done[m] <= s < done[m] + 2:
+                    for i in range((s - done[m]) * 4, (s - done[m]) * 4 + 4):
+                        turn_query_view(m, i)
+                if s == done[m] + 1:
+                    quantise_octet(m)
+                if done[m] + 2 <= s < done[m] + 4:
+                    for r in range((s - done[m] - 2) * 4, (s - done[m] - 2) * 4 + 4, PAIR):
+                        finish_pair(b, o * OCT + r, octet_mx[m], r * P, False)

@@ -24,22 +24,22 @@ T = P // NV
 G = S // T
 OCT = 8
 N_OCT = G // OCT
-T_OCTS = [(0, 0), (0, 1), (1, 0), (1, 1), (1, 2)]
-V_OCTS = [(0, 3), (0, 2), (1, 3)]
+T_OCTS = [(0, 0), (0, 1), (0, 2), (1, 0), (1, 1), (1, 2)]
+V_OCTS = [(0, 3), (1, 3)]
 ROW_OCTS = 3
 PAIR = 2
 OCT_PAIRS = OCT // PAIR
 N_PAIRS = len(T_OCTS) * OCT_PAIRS
 LEAD = 2
-UNITS = 11
+UNITS = 6
 OCT_UNITS = NV * NV
 N_UNITS = len(V_OCTS) * OCT_UNITS
 
 FLOPS = 2 * 2 * B * NV * S * D * D + 2 * B * NV * NV * S * D
 
 
-def by_head(ap):
-    return ap.rearrange("p (u h k) -> p h u k", u=2, h=H, k=HD // 2)
+def head(h):
+    return slice(h * HD, (h + 1) * HD)
 
 
 def tile_crossviewattention_pa_t_kernel(tc, x, scores, Wv, bv, Wo, bo, out):
@@ -78,8 +78,8 @@ def tile_crossviewattention_pa_t_kernel(tc, x, scores, Wv, bv, Wo, bo, out):
         wv_raw = keep.tile([P, PACK, D], BF16, name="w_raw")
         nc.scalar.dma_start(out=wv_raw[:], in_=Wv.rearrange("(p a) c -> p a c", a=PACK))
         load_x(0, 3)
-        bv_raw = keep.tile([P, D], BF16, name="bv_raw")
-        nc.scalar.dma_start(out=bv_raw[:], in_=bv.partition_broadcast(P))
+        bv_all = keep.tile([P, D], BF16, name="bv_all")
+        nc.scalar.dma_start(out=bv_all[:], in_=bv.partition_broadcast(P))
         bo_all = keep.tile([P, D], BF16, name="bo_all")
         nc.scalar.dma_start(out=bo_all[:], in_=bo.partition_broadcast(P))
 
@@ -252,25 +252,26 @@ def tile_crossviewattention_pa_t_kernel(tc, x, scores, Wv, bv, Wo, bo, out):
                 mix = ps_mix.tile([P, D], F32, name="mix")
                 for h in range(H):
                     nc.tensor.matmul(
-                        out=by_head(mix[:])[:, h, :, :],
+                        out=mix[:, head(h)],
                         lhsT=mixers[n][:, k * H + h, :, :].rearrange("p t i -> p (t i)"),
-                        rhs=by_head(v_of[(n, k)][:])[:, h, :, :],
+                        rhs=v_of[(n, k)][:, head(h)],
                         start=True,
                         stop=True,
                     )
-                nc.scalar.copy(out=mixed[:, k * D : (k + 1) * D], in_=mix[:])
+                nc.scalar.copy(
+                    out=mixed[:, k * D : (k + 1) * D].rearrange("p (u q e) -> p u q e", u=2, e=2),
+                    in_=mix[:].rearrange("p (q u e) -> p u q e", u=2, e=2),
+                )
             mixed_of[n] = mixed
-
-        def turn_mixed(words, mt):
-            for u in range(2):
-                nc.tensor.transpose(out=mt[:, u, :], in_=words[:, u * P : (u + 1) * P], identity=ident[:])
 
         def stage_turn(n):
             words = mixed_of[n][:].bitcast(F32)
             mt = ps_turn.tile([P, PAIR, 2, P], F32, tag="turn", name="mt")
             grouped = flow.tile([P, PAIR * P * PACK], BF16, name="grouped", align_bytes=64)
             for k in range(PAIR):
-                turn_mixed(words[:, k * WORDS : (k + 1) * WORDS], mt[:, k, :, :])
+                for u in range(2):
+                    first = k * WORDS + u * P
+                    nc.tensor.transpose(out=mt[:, k, u, :], in_=words[:, first : first + P], identity=ident[:])
             for k in range(PAIR):
                 nc.scalar.copy(
                     out=grouped[:].bitcast(F32).rearrange("p (k i t u) -> p k i t u", k=PAIR, i=NV, t=T, u=2)[
@@ -287,7 +288,7 @@ def tile_crossviewattention_pa_t_kernel(tc, x, scores, Wv, bv, Wo, bo, out):
             y_sb = flow.tile([P, PAIR, D], F32, name="y_sb")
             for k in range(PAIR):
                 y = project(ps_proj, operand, first + k * P, wo_mx)
-                if on_scalar:
+                if on_scalar and k == 0:
                     nc.scalar.copy(out=y_sb[:, k, :], in_=y[:])
                     nc.gpsimd.tensor_tensor(out=y_sb[:, k, :], in0=y_sb[:, k, :], in1=bo_all[:], op=ALU.add)
                 else:
@@ -319,10 +320,10 @@ def tile_crossviewattention_pa_t_kernel(tc, x, scores, Wv, bv, Wo, bo, out):
             for h in range(H):
                 col = (h * B + b) * NV + i
                 nc.vector.scalar_tensor_tensor(
-                    out=by_head(after)[:, h, :, :],
-                    in0=by_head(view_sums[k][:])[:, h, :, :],
+                    out=after[:, head(h)],
+                    in0=view_sums[k][:, head(h)],
                     scalar=w_cols[o][:, j, col : col + 1],
-                    in1=by_head(before)[:, h, :, :],
+                    in1=before[:, head(h)],
                     op0=ALU.mult,
                     op1=ALU.add,
                 )
@@ -331,7 +332,11 @@ def tile_crossviewattention_pa_t_kernel(tc, x, scores, Wv, bv, Wo, bo, out):
             if i == 0:
                 octet_grouped[m] = keep.tile([P, OCT * P * PACK], BF16, name="mgv", align_bytes=64)
             mt = ps_turn.tile([P, 2, P], F32, tag="turn", name="mtv")
-            turn_mixed(octet_mixed[m][:].bitcast(F32)[:, i * WORDS : (i + 1) * WORDS], mt[:])
+            words = octet_mixed[m][:].bitcast(F32)
+            for u in range(2):
+                nc.tensor.transpose(
+                    out=mt[:, u, :], in_=words[:, i * WORDS + u : (i + 1) * WORDS : 2], identity=ident[:]
+                )
             by_tile = octet_grouped[m][:].bitcast(F32).rearrange(
                 "p (r i t u) -> p r i t u", r=OCT, i=NV, t=T, u=2
             )
@@ -345,16 +350,9 @@ def tile_crossviewattention_pa_t_kernel(tc, x, scores, Wv, bv, Wo, bo, out):
             nc.vector.quantize_mx(out=codes[:].bitcast(FP8X4), scales=scales[:], in_=octet_grouped[m][:])
             octet_mx[m] = (codes, scales)
 
-        def quantise_weight(name, raw, permute):
+        def quantise_weight(name, raw):
             grouped = keep.tile([P, D, PACK], BF16, name="w_grouped", align_bytes=64)
-            if permute:
-                for u in range(2):
-                    nc.vector.tensor_copy(
-                        out=grouped[:].rearrange("p (u q e) a -> p u q e a", u=2, e=2)[:, u, :, :, :],
-                        in_=raw[:].rearrange("p a (q u e) -> p u q e a", u=2, e=2)[:, u, :, :, :],
-                    )
-            else:
-                nc.vector.tensor_copy(out=grouped[:], in_=raw[:].rearrange("p a c -> p c a"))
+            nc.vector.tensor_copy(out=grouped[:], in_=raw[:].rearrange("p a c -> p c a"))
             codes = keep.tile([P, D], U32, name=name + "_codes", align_bytes=64)
             scales = keep.tile([P, D], U8, name=name + "_scales", align_bytes=64)
             nc.vector.quantize_mx(
@@ -364,12 +362,7 @@ def tile_crossviewattention_pa_t_kernel(tc, x, scores, Wv, bv, Wo, bo, out):
 
         HALF = OCT // 2
         exponentials(0, 0, HALF)
-        wv_mx = quantise_weight("wv", wv_raw, True)
-        bv_all = keep.tile([P, D], BF16, name="bv_all")
-        nc.vector.tensor_copy(
-            out=bv_all[:].rearrange("p (u q e) -> p u q e", u=2, e=2),
-            in_=bv_raw[:].rearrange("p (q u e) -> p u q e", u=2, e=2),
-        )
+        wv_mx = quantise_weight("wv", wv_raw)
         prepare_pair(0)
         normalise(0, 0, HALF)
         row_weights(0, 0, HALF)
@@ -385,12 +378,14 @@ def tile_crossviewattention_pa_t_kernel(tc, x, scores, Wv, bv, Wo, bo, out):
         project_view(0)
         load_x(0, 1)
         load_x(0, 2)
+        wo_raw = keep.tile([P, PACK, D], BF16, name="w_raw")
+        nc.sync.dma_start(out=wo_raw[:], in_=Wo.rearrange("(p a) c -> p a c", a=PACK))
         exponentials(0, HALF, HALF)
         normalise(0, HALF, HALF)
         row_weights(0, HALF, HALF)
 
         done = [-(-(m + 1) * OCT_UNITS // UNITS) for m in range(len(V_OCTS))]
-        view_steps = {first + k: (m, k * PAIR) for m, first in ((1, 2), (2, 7)) for k in range(OCT_PAIRS)}
+        view_steps = {first + k: (m, k * PAIR) for m, first in ((1, 6),) for k in range(OCT_PAIRS)}
         n_steps = N_PAIRS + 2
         for s in range(n_steps):
             if s + 2 < N_PAIRS:
@@ -402,15 +397,14 @@ def tile_crossviewattention_pa_t_kernel(tc, x, scores, Wv, bv, Wo, bo, out):
             if s == 1:
                 load_x(1, 0)
                 load_x(1, 3)
-            if s == 5:
+            if s == 6:
                 load_x(1, 1)
+            if s == 10:
                 load_x(1, 2)
             if s + 1 < N_PAIRS:
                 stage_v(s + 1)
             if s == 0:
-                wo_raw = keep.tile([P, PACK, D], BF16, name="w_raw")
-                nc.scalar.dma_start(out=wo_raw[:], in_=Wo.rearrange("(p a) c -> p a c", a=PACK))
-                wo_mx = quantise_weight("wo", wo_raw, False)
+                wo_mx = quantise_weight("wo", wo_raw)
             if 0 <= s - 2 < N_PAIRS:
                 n = s - 2
                 b, o = T_OCTS[n // OCT_PAIRS]
@@ -426,7 +420,6 @@ def tile_crossviewattention_pa_t_kernel(tc, x, scores, Wv, bv, Wo, bo, out):
             if s == 3:
                 exponentials(2)
                 normalise(2)
-                col_weights(2)
                 row_weights(2)
             for n in range(s * UNITS, min((s + 1) * UNITS, N_UNITS)):
                 add_unit(n)

@@ -29,8 +29,8 @@ V_OCTS = [(0, 3), (1, 3)]
 ROW_OCTS = 3
 PAIR = 2
 OCT_PAIRS = OCT // PAIR
+QUAD = 4
 N_PAIRS = len(T_OCTS) * OCT_PAIRS
-LEAD = 2
 UNITS = 6
 OCT_UNITS = NV * NV
 N_UNITS = len(V_OCTS) * OCT_UNITS
@@ -50,8 +50,9 @@ def tile_crossviewattention_pa_t_kernel(tc, x, scores, Wv, bv, Wo, bo, out):
     with ExitStack() as stack:
         keep = stack.enter_context(tc.tile_pool(name="keep", bufs=1))
         soft = stack.enter_context(tc.tile_pool(name="soft", bufs=2))
-        xin = stack.enter_context(tc.tile_pool(name="xin", bufs=4))
+        xin = stack.enter_context(tc.tile_pool(name="xin", bufs=3))
         flow = stack.enter_context(tc.tile_pool(name="flow", bufs=3))
+        mixer_pool = stack.enter_context(tc.tile_pool(name="mixer_pool", bufs=2))
         values = stack.enter_context(tc.tile_pool(name="values", bufs=6))
         ps_view = stack.enter_context(tc.psum_pool(name="ps_view", bufs=2))
         ps_proj = stack.enter_context(tc.psum_pool(name="ps_proj", bufs=2))
@@ -214,36 +215,37 @@ def tile_crossviewattention_pa_t_kernel(tc, x, scores, Wv, bv, Wo, bo, out):
         mixed_of = {}
         m_mx_of = {}
 
-        def stage_mixers(n):
-            b, o = T_OCTS[n // OCT_PAIRS]
-            g = o * OCT + n % OCT_PAIRS * PAIR
-            w = w_by_scene[:, b, g * H : (g + PAIR) * H, :]
-            mixer = flow.tile([P, PAIR * H, T, NV], F32, name="mixer")
-            if n % 2 == 0:
-                for k in range(PAIR):
-                    heads = slice(k * H, (k + 1) * H)
-                    nc.gpsimd.tensor_tensor(
-                        out=mixer[:, heads, :, :],
-                        in0=w[:, heads, :].unsqueeze(2).to_broadcast([P, H, T, NV]),
-                        in1=same_t[:].unsqueeze(1).unsqueeze(3).to_broadcast([P, H, T, NV]),
-                        op=ALU.mult,
-                    )
-            else:
-                for t in range(T):
-                    nc.scalar.activation(
-                        out=mixer[:, :, t, :],
-                        in_=w,
-                        func=ACT.Copy,
-                        scale=same_t[:, t : t + 1],
-                    )
-            mixers[n] = mixer
+        def quad_weights(q):
+            b, o = T_OCTS[q * QUAD // OCT]
+            g = o * OCT + q * QUAD % OCT
+            return w_by_scene[:, b, g * H : (g + QUAD) * H, :]
+
+        def mixers_gpsimd(q):
+            w = quad_weights(q)
+            mixers[q] = mixer_pool.tile([P, QUAD * H, T, NV], F32, name="mixer")
+            for k in range(QUAD):
+                heads = slice(k * H, (k + 1) * H)
+                nc.gpsimd.tensor_tensor(
+                    out=mixers[q][:, heads, :, :],
+                    in0=w[:, heads, :].unsqueeze(2).to_broadcast([P, H, T, NV]),
+                    in1=same_t[:].unsqueeze(1).unsqueeze(3).to_broadcast([P, H, T, NV]),
+                    op=ALU.mult,
+                )
+
+        def mixers_scalar(q, t0):
+            w = quad_weights(q)
+            if t0 == 0:
+                mixers[q] = mixer_pool.tile([P, QUAD * H, T, NV], F32, name="mixer")
+            for t in range(t0, t0 + T // 2):
+                nc.scalar.activation(
+                    out=mixers[q][:, :, t, :], in_=w, func=ACT.Copy, scale=same_t[:, t : t + 1]
+                )
 
         def stage_v(n):
             for k in range(PAIR):
                 v = project(ps_proj, x_mx[n], k * P, wv_mx)
                 v_sb = values.tile([P, D], F32, name="v_sb")
-                nc.scalar.copy(out=v_sb[:], in_=v[:])
-                nc.gpsimd.tensor_tensor(out=v_sb[:], in0=v_sb[:], in1=bv_all[:], op=ALU.add)
+                nc.vector.tensor_tensor(out=v_sb[:], in0=v[:], in1=bv_all[:], op=ALU.add)
                 v_of[(n, k)] = v_sb
 
         def stage_mix(n):
@@ -253,7 +255,7 @@ def tile_crossviewattention_pa_t_kernel(tc, x, scores, Wv, bv, Wo, bo, out):
                 for h in range(H):
                     nc.tensor.matmul(
                         out=mix[:, head(h)],
-                        lhsT=mixers[n][:, k * H + h, :, :].rearrange("p t i -> p (t i)"),
+                        lhsT=mixers[n // 2][:, (n % 2 * PAIR + k) * H + h, :, :].rearrange("p t i -> p (t i)"),
                         rhs=v_of[(n, k)][:, head(h)],
                         start=True,
                         stop=True,
@@ -366,8 +368,7 @@ def tile_crossviewattention_pa_t_kernel(tc, x, scores, Wv, bv, Wo, bo, out):
         prepare_pair(0)
         normalise(0, 0, HALF)
         row_weights(0, 0, HALF)
-        for n in range(LEAD):
-            stage_mixers(n)
+        mixers_gpsimd(0)
         stage_v(0)
         exponentials(3)
         prepare_pair(1)
@@ -377,7 +378,6 @@ def tile_crossviewattention_pa_t_kernel(tc, x, scores, Wv, bv, Wo, bo, out):
         col_weights(3)
         project_view(0)
         load_x(0, 1)
-        load_x(0, 2)
         wo_raw = keep.tile([P, PACK, D], BF16, name="w_raw")
         nc.sync.dma_start(out=wo_raw[:], in_=Wo.rearrange("(p a) c -> p a c", a=PACK))
         exponentials(0, HALF, HALF)
@@ -395,11 +395,12 @@ def tile_crossviewattention_pa_t_kernel(tc, x, scores, Wv, bv, Wo, bo, out):
             if 0 <= s - 1 < N_PAIRS:
                 stage_turn(s - 1)
             if s == 1:
-                load_x(1, 0)
+                load_x(0, 2)
                 load_x(1, 3)
-            if s == 6:
+            if s == 5:
+                load_x(1, 0)
+            if s == 9:
                 load_x(1, 1)
-            if s == 10:
                 load_x(1, 2)
             if s + 1 < N_PAIRS:
                 stage_v(s + 1)
@@ -409,8 +410,8 @@ def tile_crossviewattention_pa_t_kernel(tc, x, scores, Wv, bv, Wo, bo, out):
                 n = s - 2
                 b, o = T_OCTS[n // OCT_PAIRS]
                 finish_pair(b, o * OCT + n % OCT_PAIRS * PAIR, m_mx_of[n], 0, True)
-            if s + LEAD < N_PAIRS:
-                stage_mixers(s + LEAD)
+            if (s // 2 + 1) * QUAD < N_PAIRS * PAIR:
+                mixers_scalar(s // 2 + 1, s % 2 * T // 2)
             if s < N_PAIRS:
                 stage_mix(s)
             if s == 0:

@@ -31,7 +31,7 @@ PAIR = 2
 OCT_PAIRS = OCT // PAIR
 QUAD = 4
 N_PAIRS = len(T_OCTS) * OCT_PAIRS
-UNITS = 6
+UNITS = 7
 OCT_UNITS = NV * NV
 N_UNITS = len(V_OCTS) * OCT_UNITS
 
@@ -245,7 +245,11 @@ def tile_crossviewattention_pa_t_kernel(tc, x, scores, Wv, bv, Wo, bo, out):
             for k in range(PAIR):
                 v = project(ps_proj, x_mx[n], k * P, wv_mx)
                 v_sb = values.tile([P, D], F32, name="v_sb")
-                nc.vector.tensor_tensor(out=v_sb[:], in0=v[:], in1=bv_all[:], op=ALU.add)
+                if n < QUAD // PAIR:
+                    nc.vector.tensor_tensor(out=v_sb[:], in0=v[:], in1=bv_all[:], op=ALU.add)
+                else:
+                    nc.scalar.copy(out=v_sb[:], in_=v[:])
+                    nc.gpsimd.tensor_tensor(out=v_sb[:], in0=v_sb[:], in1=bv_all[:], op=ALU.add)
                 v_of[(n, k)] = v_sb
 
         def stage_mix(n):
@@ -385,7 +389,7 @@ def tile_crossviewattention_pa_t_kernel(tc, x, scores, Wv, bv, Wo, bo, out):
         row_weights(0, HALF, HALF)
 
         done = [-(-(m + 1) * OCT_UNITS // UNITS) for m in range(len(V_OCTS))]
-        view_steps = {first + k: (m, k * PAIR) for m, first in ((1, 6),) for k in range(OCT_PAIRS)}
+        view_steps = {first + k: (m, k * PAIR) for m, first in ((1, 5),) for k in range(OCT_PAIRS)}
         n_steps = N_PAIRS + 2
         for s in range(n_steps):
             if s + 2 < N_PAIRS:
@@ -409,7 +413,7 @@ def tile_crossviewattention_pa_t_kernel(tc, x, scores, Wv, bv, Wo, bo, out):
             if 0 <= s - 2 < N_PAIRS:
                 n = s - 2
                 b, o = T_OCTS[n // OCT_PAIRS]
-                finish_pair(b, o * OCT + n % OCT_PAIRS * PAIR, m_mx_of[n], 0, True)
+                finish_pair(b, o * OCT + n % OCT_PAIRS * PAIR, m_mx_of[n], 0, n + 2 < N_PAIRS)
             if (s // 2 + 1) * QUAD < N_PAIRS * PAIR:
                 mixers_scalar(s // 2 + 1, s % 2 * T // 2)
             if s < N_PAIRS:
@@ -426,11 +430,10 @@ def tile_crossviewattention_pa_t_kernel(tc, x, scores, Wv, bv, Wo, bo, out):
                 add_unit(n)
             for m in range(len(V_OCTS)):
                 b, o = V_OCTS[m]
-                if done[m] <= s < done[m] + 2:
-                    for i in range((s - done[m]) * 4, (s - done[m]) * 4 + 4):
+                if s == done[m]:
+                    for i in range(NV):
                         turn_query_view(m, i)
-                if s == done[m] + 1:
                     quantise_octet(m)
-                if done[m] + 2 <= s < done[m] + 4:
-                    for r in range((s - done[m] - 2) * 4, (s - done[m] - 2) * 4 + 4, PAIR):
+                if done[m] < s < done[m] + 3:
+                    for r in range((s - done[m] - 1) * 4, (s - done[m]) * 4, PAIR):
                         finish_pair(b, o * OCT + r, octet_mx[m], r * P, False)

from contextlib import ExitStack

import concourse.mybir as mybir
from concourse.masks import make_identity

F32 = mybir.dt.float32
BF16 = mybir.dt.bfloat16
U32 = mybir.dt.uint32
U8 = mybir.dt.uint8
FP8X4 = mybir.dt.float8_e4m3fn_x4
ALU = mybir.AluOpType
ACT = mybir.ActivationFunctionType

P = 128
PACK = 4
B = 2
NV = 8
S = 512
D = 512
WORDS = D // 2
H = 8
HD = D // H
T = P // NV
G = S // T
OCT = 8
N_OCT = G // OCT
T_OCTS = [(0, 0), (0, 1), (0, 2), (1, 0), (1, 1), (1, 2)]
V_OCTS = [(0, 3), (1, 3)]
ROW_OCTS = 3
PAIR = 2
OCT_PAIRS = OCT // PAIR
QUAD = 4
N_PAIRS = len(T_OCTS) * OCT_PAIRS
UNITS = 7
OCT_UNITS = NV * NV
N_UNITS = len(V_OCTS) * OCT_UNITS

FLOPS = 2 * 2 * B * NV * S * D * D + 2 * B * NV * NV * S * D


def head(h):
    return slice(h * HD, (h + 1) * HD)


def tile_crossviewattention_pa_t_kernel(tc, x, scores, Wv, bv, Wo, bo, out):
    nc = tc.nc
    x_tiles = x.flatten_outer_dims().rearrange("(b p g) d -> b p g d", b=B, p=P, g=G)
    out_tiles = out.flatten_outer_dims().rearrange("(b p g) d -> b p g d", b=B, p=P, g=G)

    with ExitStack() as stack:
        keep = stack.enter_context(tc.tile_pool(name="keep", bufs=1))
        soft = stack.enter_context(tc.tile_pool(name="soft", bufs=2))
        xin = stack.enter_context(tc.tile_pool(name="xin", bufs=3))
        flow = stack.enter_context(tc.tile_pool(name="flow", bufs=3))
        mixer_pool = stack.enter_context(tc.tile_pool(name="mixer_pool", bufs=2))
        values = stack.enter_context(tc.tile_pool(name="values", bufs=6))
        ps_view = stack.enter_context(tc.psum_pool(name="ps_view", bufs=2))
        ps_proj = stack.enter_context(tc.psum_pool(name="ps_proj", bufs=2))
        ps_mix = stack.enter_context(tc.psum_pool(name="ps_mix", bufs=2))
        ps_turn = stack.enter_context(tc.psum_pool(name="ps_turn", bufs=2))

        raw_scores = keep.tile([P, NV, S], BF16, name="raw_scores")
        for h in range(H):
            nc.sync.dma_start(
                out=raw_scores[h * B * NV : (h + 1) * B * NV, :, :],
                in_=scores[:, :, :, h, :].rearrange("b i j s -> (b i) j s"),
            )
        x_in = {}

        def load_x(b, o):
            x_oct = xin.tile([P, OCT * D], BF16, name="x_oct")
            nc.sync.dma_start(
                out=x_oct[:],
                in_=x_tiles[b, :, o * OCT : (o + 1) * OCT, :].rearrange("p r d -> p (r d)"),
            )
            x_in[(b, o)] = x_oct

        load_x(0, 0)
        wv_raw = keep.tile([P, PACK, D], BF16, name="w_raw")
        nc.scalar.dma_start(out=wv_raw[:], in_=Wv.rearrange("(p a) c -> p a c", a=PACK))
        load_x(0, 3)
        bv_all = keep.tile([P, D], BF16, name="bv_all")
        nc.scalar.dma_start(out=bv_all[:], in_=bv.partition_broadcast(P))
        bo_all = keep.tile([P, D], BF16, name="bo_all")
        nc.scalar.dma_start(out=bo_all[:], in_=bo.partition_broadcast(P))

        ident = keep.tile([P, P], F32, name="ident")
        make_identity(nc, ident[:])
        same_t = keep.tile([P, T], F32, name="same_t")
        nc.vector.tensor_reduce(
            out=same_t[:],
            in_=ident[:].rearrange("p (j t) -> p t j", j=NV, t=T),
            axis=mybir.AxisListType.X,
            op=ALU.add,
        )

        exps = {}

        def exponentials(o, r0=0, nr=OCT):
            part = raw_scores[:].rearrange("p j (t o r) -> p o j t r", t=T, o=N_OCT, r=OCT)[
                :, o, :, :, r0 : r0 + nr
            ]
            top = soft.tile([P, NV // 2, T, nr], BF16, name="top")
            nc.vector.tensor_max(out=top[:], in0=part[:, 0:4, :, :], in1=part[:, 4:8, :, :])
            nc.vector.tensor_max(out=top[:, 0:2, :, :], in0=top[:, 0:2, :, :], in1=top[:, 2:4, :, :])
            nc.vector.tensor_max(out=top[:, 0:1, :, :], in0=top[:, 0:1, :, :], in1=top[:, 1:2, :, :])
            e = soft.tile([P, NV, T, nr], F32, name="e")
            nc.vector.tensor_tensor(
                out=e[:], in0=part, in1=top[:, 0:1, :, :].to_broadcast([P, NV, T, nr]), op=ALU.subtract
            )
            nc.scalar.activation(out=e[:], in_=e[:], func=ACT.Exp)
            exps[(o, r0)] = e

        w_rows = keep.tile([P, ROW_OCTS * OCT, P], F32, name="w_rows")
        w_by_scene = w_rows[:].rearrange("p g (h b i) -> p b (g h) i", h=H, b=B, i=NV)
        w_cols = {}
        totals = {}

        def normalise(o, r0=0, nr=OCT):
            e = exps[(o, r0)]
            total = soft.tile([P, NV // 2, T, nr], F32, name="total")
            nc.vector.tensor_add(out=total[:], in0=e[:, 0:4, :, :], in1=e[:, 4:8, :, :])
            nc.vector.tensor_add(out=total[:, 0:2, :, :], in0=total[:, 0:2, :, :], in1=total[:, 2:4, :, :])
            nc.vector.tensor_add(out=total[:, 0:1, :, :], in0=total[:, 0:1, :, :], in1=total[:, 1:2, :, :])
            nc.vector.reciprocal(out=total[:, 0:1, :, :], in_=total[:, 0:1, :, :])
            totals[(o, r0)] = total

        def weights(o, r0, order, shape, turned):
            w = soft.tile(shape, F32, name="w")
            nc.vector.tensor_tensor(
                out=w[:],
                in0=exps[(o, r0)][:].rearrange("p j t r -> p " + order),
                in1=totals[(o, r0)][:, 0:1, :, :].rearrange("p j t r -> p " + order).to_broadcast(shape),
                op=ALU.mult,
            )
            for first in range(0, shape[1], 4):
                wt = ps_turn.tile([P, 4, P], F32, tag="turn", name="wt")
                for k in range(4):
                    nc.tensor.transpose(
                        out=wt[:, k, :],
                        in_=w[:, first + k, :, :].rearrange("p m n -> p (m n)"),
                        identity=ident[:],
                    )
                nc.scalar.copy(out=turned[:, first : first + 4, :], in_=wt[:])

        def row_weights(o, r0=0, nr=OCT):
            weights(o, r0, "r j t", [P, nr, NV, T], w_rows[:, o * OCT + r0 : o * OCT + r0 + nr, :])

        def col_weights(o):
            w_cols[o] = keep.tile([P, NV, P], F32, name="w_cols_" + str(o))
            weights(o, 0, "j r t", [P, NV, OCT, T], w_cols[o][:])

        x_mx = {}
        view_xg = {}

        def turn_x(b, o, r0):
            words = x_in[(b, o)][:].bitcast(F32)
            xt = ps_turn.tile([P, PAIR, 2, P], F32, tag="turn", name="xt")
            for k in range(PAIR):
                for u in range(2):
                    first = (r0 + k) * WORDS
                    nc.tensor.transpose(
                        out=xt[:, k, u, :], in_=words[:, first + u : first + WORDS : 2], identity=ident[:]
                    )
            return xt

        def prepare_pair(n):
            b, o = T_OCTS[n // OCT_PAIRS]
            xt = turn_x(b, o, n % OCT_PAIRS * PAIR)
            xg = flow.tile([P, PAIR * P * PACK], BF16, name="xg", align_bytes=64)
            nc.scalar.copy(
                out=xg[:].bitcast(F32).rearrange("p (k n u) -> p k n u", k=PAIR, n=P, u=2),
                in_=xt[:].rearrange("p k u n -> p k n u"),
            )
            codes = flow.tile([P, PAIR * P], U32, name="x_codes", align_bytes=64)
            scales = flow.tile([P, PAIR * P], U8, name="x_scales", align_bytes=64)
            nc.vector.quantize_mx(out=codes[:].bitcast(FP8X4), scales=scales[:], in_=xg[:])
            x_mx[n] = (codes, scales)

        def prepare_views(m, r0):
            b, o = V_OCTS[m]
            if r0 == 0:
                view_xg[m] = keep.tile([P, OCT * P * PACK], BF16, name="view_xg", align_bytes=64)
            by_view = view_xg[m][:].bitcast(F32).rearrange("p (j r t u) -> p j r t u", j=NV, r=OCT, t=T, u=2)
            xt = turn_x(b, o, r0)
            for k in range(PAIR):
                nc.scalar.copy(
                    out=by_view[:, :, r0 + k, :, :],
                    in_=xt[:, k, :, :].rearrange("p u (j t) -> p j t u", j=NV, t=T),
                )
            if r0 + PAIR == OCT:
                codes = soft.tile([P, OCT * P], U32, name="view_codes", align_bytes=64)
                scales = soft.tile([P, OCT * P], U8, name="view_scales", align_bytes=64)
                nc.vector.quantize_mx(out=codes[:].bitcast(FP8X4), scales=scales[:], in_=view_xg[m][:])
                x_mx[("view", m)] = (codes, scales)

        def project(pool, operand, first, weight):
            codes, scales = operand
            w_codes, w_scales = weight
            tokens = slice(first, first + P)
            sums = pool.tile([P, D], F32, name="sums")
            nc.tensor.matmul_mx(
                out=sums[:],
                lhsT=codes[:, tokens].bitcast(FP8X4),
                lhsT_scale=scales[:, tokens],
                rhs=w_codes[:].bitcast(FP8X4),
                rhs_scale=w_scales[:],
                start=True,
                stop=True,
            )
            return sums

        mixers = {}
        v_of = {}
        mixed_of = {}
        m_mx_of = {}

        def quad_weights(q):
            b, o = T_OCTS[q * QUAD // OCT]
            g = o * OCT + q * QUAD % OCT
            return w_by_scene[:, b, g * H : (g + QUAD) * H, :]

        def mixers_gpsimd(q):
            w = quad_weights(q)
            mixers[q] = mixer_pool.tile([P, QUAD * H, T, NV], F32, name="mixer")
            for k in range(QUAD):
                heads = slice(k * H, (k + 1) * H)
                nc.gpsimd.tensor_tensor(
                    out=mixers[q][:, heads, :, :],
                    in0=w[:, heads, :].unsqueeze(2).to_broadcast([P, H, T, NV]),
                    in1=same_t[:].unsqueeze(1).unsqueeze(3).to_broadcast([P, H, T, NV]),
                    op=ALU.mult,
                )

        def mixers_scalar(q, t0):
            w = quad_weights(q)
            if t0 == 0:
                mixers[q] = mixer_pool.tile([P, QUAD * H, T, NV], F32, name="mixer")
            for t in range(t0, t0 + T // 2):
                nc.scalar.activation(
                    out=mixers[q][:, :, t, :], in_=w, func=ACT.Copy, scale=same_t[:, t : t + 1]
                )

        def stage_v(n):
            for k in range(PAIR):
                v = project(ps_proj, x_mx[n], k * P, wv_mx)
                v_sb = values.tile([P, D], F32, name="v_sb")
                if n < QUAD // PAIR:
                    nc.vector.tensor_tensor(out=v_sb[:], in0=v[:], in1=bv_all[:], op=ALU.add)
                else:
                    nc.scalar.copy(out=v_sb[:], in_=v[:])
                    nc.gpsimd.tensor_tensor(out=v_sb[:], in0=v_sb[:], in1=bv_all[:], op=ALU.add)
                v_of[(n, k)] = v_sb

        def stage_mix(n):
            mixed = flow.tile([P, PAIR * D], BF16, name="mixed")
            for k in range(PAIR):
                mix = ps_mix.tile([P, D], F32, name="mix")
                for h in range(H):
                    nc.tensor.matmul(
                        out=mix[:, head(h)],
                        lhsT=mixers[n // 2][:, (n % 2 * PAIR + k) * H + h, :, :].rearrange("p t i -> p (t i)"),
                        rhs=v_of[(n, k)][:, head(h)],
                        start=True,
                        stop=True,
                    )
                nc.scalar.copy(
                    out=mixed[:, k * D : (k + 1) * D].rearrange("p (u q e) -> p u q e", u=2, e=2),
                    in_=mix[:].rearrange("p (q u e) -> p u q e", u=2, e=2),
                )
            mixed_of[n] = mixed

        def stage_turn(n):
            words = mixed_of[n][:].bitcast(F32)
            mt = ps_turn.tile([P, PAIR, 2, P], F32, tag="turn", name="mt")
            grouped = flow.tile([P, PAIR * P * PACK], BF16, name="grouped", align_bytes=64)
            for k in range(PAIR):
                for u in range(2):
                    first = k * WORDS + u * P
                    nc.tensor.transpose(out=mt[:, k, u, :], in_=words[:, first : first + P], identity=ident[:])
            for k in range(PAIR):
                nc.scalar.copy(
                    out=grouped[:].bitcast(F32).rearrange("p (k i t u) -> p k i t u", k=PAIR, i=NV, t=T, u=2)[
                        :, k, :, :, :
                    ],
                    in_=mt[:, k, :, :].rearrange("p u (t i) -> p i t u", t=T, i=NV),
                )
            codes = flow.tile([P, PAIR * P], U32, name="m_codes", align_bytes=64)
            scales = flow.tile([P, PAIR * P], U8, name="m_scales", align_bytes=64)
            nc.vector.quantize_mx(out=codes[:].bitcast(FP8X4), scales=scales[:], in_=grouped[:])
            m_mx_of[n] = (codes, scales)

        def finish_pair(b, g, operand, first, on_scalar):
            y_sb = flow.tile([P, PAIR, D], F32, name="y_sb")
            for k in range(PAIR):
                y = project(ps_proj, operand, first + k * P, wo_mx)
                if on_scalar and k == 0:
                    nc.scalar.copy(out=y_sb[:, k, :], in_=y[:])
                    nc.gpsimd.tensor_tensor(out=y_sb[:, k, :], in0=y_sb[:, k, :], in1=bo_all[:], op=ALU.add)
                else:
                    nc.vector.tensor_tensor(out=y_sb[:, k, :], in0=y[:], in1=bo_all[:], op=ALU.add)
            nc.sync.dma_start(out=out_tiles[b, :, g : g + PAIR, :], in_=y_sb[:])

        view_sums = {}
        octet_sums = {}
        octet_mixed = {}
        octet_grouped = {}
        octet_mx = {}

        def project_view(k):
            m, j = divmod(k, NV)
            view_sums[k] = project(ps_view, x_mx[("view", m)], j * P, wv_mx)

        def add_unit(n):
            k, i = divmod(n, NV)
            m, j = divmod(k, NV)
            b, o = V_OCTS[m]
            if i == 0 and j == 0:
                octet_sums[m] = keep.tile([P, NV, D], F32, name="acc")
            if i == 0 and j == NV - 1:
                octet_mixed[m] = keep.tile([P, NV * D], BF16, name="mixed_v")
            if i == 0 and n + NV < N_UNITS:
                project_view(k + 1)
            before = bv_all[:] if j == 0 else octet_sums[m][:, i, :]
            after = octet_mixed[m][:, i * D : (i + 1) * D] if j == NV - 1 else octet_sums[m][:, i, :]
            for h in range(H):
                col = (h * B + b) * NV + i
                nc.vector.scalar_tensor_tensor(
                    out=after[:, head(h)],
                    in0=view_sums[k][:, head(h)],
                    scalar=w_cols[o][:, j, col : col + 1],
                    in1=before[:, head(h)],
                    op0=ALU.mult,
                    op1=ALU.add,
                )

        def turn_query_view(m, i):
            if i == 0:
                octet_grouped[m] = keep.tile([P, OCT * P * PACK], BF16, name="mgv", align_bytes=64)
            mt = ps_turn.tile([P, 2, P], F32, tag="turn", name="mtv")
            words = octet_mixed[m][:].bitcast(F32)
            for u in range(2):
                nc.tensor.transpose(
                    out=mt[:, u, :], in_=words[:, i * WORDS + u : (i + 1) * WORDS : 2], identity=ident[:]
                )
            by_tile = octet_grouped[m][:].bitcast(F32).rearrange(
                "p (r i t u) -> p r i t u", r=OCT, i=NV, t=T, u=2
            )
            nc.scalar.copy(
                out=by_tile[:, :, i, :, :], in_=mt[:].rearrange("p u (r t) -> p r t u", r=OCT, t=T)
            )

        def quantise_octet(m):
            codes = keep.tile([P, OCT * P], U32, name="mv_codes", align_bytes=64)
            scales = keep.tile([P, OCT * P], U8, name="mv_scales", align_bytes=64)
            nc.vector.quantize_mx(out=codes[:].bitcast(FP8X4), scales=scales[:], in_=octet_grouped[m][:])
            octet_mx[m] = (codes, scales)

        def quantise_weight(name, raw):
            grouped = keep.tile([P, D, PACK], BF16, name="w_grouped", align_bytes=64)
            nc.vector.tensor_copy(out=grouped[:], in_=raw[:].rearrange("p a c -> p c a"))
            codes = keep.tile([P, D], U32, name=name + "_codes", align_bytes=64)
            scales = keep.tile([P, D], U8, name=name + "_scales", align_bytes=64)
            nc.vector.quantize_mx(
                out=codes[:].bitcast(FP8X4), scales=scales[:], in_=grouped[:].rearrange("p c a -> p (c a)")
            )
            return codes, scales

        HALF = OCT // 2
        exponentials(0, 0, HALF)
        wv_mx = quantise_weight("wv", wv_raw)
        prepare_pair(0)
        normalise(0, 0, HALF)
        row_weights(0, 0, HALF)
        mixers_gpsimd(0)
        stage_v(0)
        exponentials(3)
        prepare_pair(1)
        for r0 in range(0, OCT, PAIR):
            prepare_views(0, r0)
        normalise(3)
        col_weights(3)
        project_view(0)
        load_x(0, 1)
        wo_raw = keep.tile([P, PACK, D], BF16, name="w_raw")
        nc.sync.dma_start(out=wo_raw[:], in_=Wo.rearrange("(p a) c -> p a c", a=PACK))
        exponentials(0, HALF, HALF)
        normalise(0, HALF, HALF)
        row_weights(0, HALF, HALF)

        done = [-(-(m + 1) * OCT_UNITS // UNITS) for m in range(len(V_OCTS))]
        view_steps = {first + k: (m, k * PAIR) for m, first in ((1, 5),) for k in range(OCT_PAIRS)}
        n_steps = N_PAIRS + 2
        for s in range(n_steps):
            if s + 2 < N_PAIRS:
                prepare_pair(s + 2)
            if s in view_steps:
                prepare_views(*view_steps[s])
            if 0 <= s - 1 < N_PAIRS:
                stage_turn(s - 1)
            if s == 1:
                load_x(0, 2)
                load_x(1, 3)
            if s == 5:
                load_x(1, 0)
            if s == 9:
                load_x(1, 1)
                load_x(1, 2)
            if s + 1 < N_PAIRS:
                stage_v(s + 1)
            if s == 0:
                wo_mx = quantise_weight("wo", wo_raw)
            if 0 <= s - 2 < N_PAIRS:
                n = s - 2
                b, o = T_OCTS[n // OCT_PAIRS]
                finish_pair(b, o * OCT + n % OCT_PAIRS * PAIR, m_mx_of[n], 0, n + 2 < N_PAIRS)
            if (s // 2 + 1) * QUAD < N_PAIRS * PAIR:
                mixers_scalar(s // 2 + 1, s % 2 * T // 2)
            if s < N_PAIRS:
                stage_mix(s)
            if s == 0:
                exponentials(1)
                normalise(1)
                row_weights(1)
            if s == 3:
                exponentials(2)
                normalise(2)
                row_weights(2)
            for n in range(s * UNITS, min((s + 1) * UNITS, N_UNITS)):
                add_unit(n)
            for m in range(len(V_OCTS)):
                b, o = V_OCTS[m]
                if s == done[m]:
                    for i in range(NV):
                        turn_query_view(m, i)
                    quantise_octet(m)
                if done[m] < s < done[m] + 3:
                    for r in range((s - done[m] - 1) * 4, (s - done[m]) * 4, PAIR):
                        finish_pair(b, o * OCT + r, octet_mx[m], r * P, False)
